import numpy as np
import ml_dtypes


def mxq(x, axis, fmt="e4m3"):
    dtype, down = {"e4m3": (ml_dtypes.float8_e4m3fn, 7), "e5m2": (ml_dtypes.float8_e5m2, 14)}[fmt]
    v = np.moveaxis(np.asarray(x, np.float32).astype(ml_dtypes.bfloat16).astype(np.float64), axis, -1)
    blocks = v.reshape(v.shape[:-1] + (-1, 32))
    amax = np.abs(blocks).max(-1, keepdims=True)
    byte = np.maximum(np.where(amax > 0, np.frexp(amax)[1] - 1 + 127, 0) - down, 1)
    scale = np.exp2(byte - 127.0)
    codes = (blocks / scale).astype(np.float32).astype(dtype).astype(np.float64)
    return np.moveaxis((codes * scale).reshape(v.shape), -1, axis)


WIDE = False


def mx_kscale(k):
    if not WIDE:
        return np.ones(k)
    levels = np.array([10, -10, 5, -5, 0])
    a = np.random.permutation(np.resize(levels, k // 512 * 4)).reshape(k // 512, 4)
    idx = np.arange(k)
    return np.exp2(a[idx // 512, idx % 128 // 32])


BF16 = ml_dtypes.bfloat16


def bf(x):
    return np.asarray(x, np.float32).astype(BF16)


def f64(x):
    return np.asarray(x).astype(np.float64)


E2M1 = np.array([0.0, 0.5, 1.0, 1.5, 2.0, 3.0, 4.0, 6.0, -0.0, -0.5, -1.0, -1.5, -2.0, -3.0, -4.0, -6.0])


def pack_weight(w, fmt):
    k, n = w.shape
    w = f64(bf(w)).reshape(k // 32, 32, n)
    amax = np.abs(w).max(1)
    if fmt == "e4m3":
        byte = np.frexp(amax)[1] - 1 + 127 - 7
    else:
        mant, ex = np.frexp(amax / 6.0)
        byte = np.where(mant > 0.5, ex, ex - 1) + 127
    byte = np.clip(np.where(amax > 0, byte, 1), 1, 254)
    scaled = (w * np.exp2(127.0 - byte)[:, None, :]).reshape(k, n).astype(np.float32)
    by_word = np.ascontiguousarray(scaled.reshape(k // 512, 128, 4, n).transpose(0, 1, 3, 2))
    if fmt == "e4m3":
        words = by_word.astype(ml_dtypes.float8_e4m3fn).view(np.uint8)
    else:
        c = by_word.astype(ml_dtypes.float4_e2m1fn).view(np.uint8) & 0xF
        words = c[..., 0::2] | (c[..., 1::2] << 4)
    return np.ascontiguousarray(words), np.ascontiguousarray(byte.astype(np.uint8).reshape(k // 512, 16, n))


def unpack_weight(words, scales, fmt):
    g, p, n, _ = words.shape
    if fmt == "e4m3":
        vals = np.ascontiguousarray(words).view(ml_dtypes.float8_e4m3fn).astype(np.float64)
    else:
        nib = np.empty((g, p, n, 4), np.uint8)
        nib[..., 0::2] = words & 0xF
        nib[..., 1::2] = words >> 4
        vals = E2M1[nib]
    vals = vals * np.repeat(np.exp2(scales.astype(np.float64) - 127.0), 8, axis=1)[..., None]
    return vals.transpose(0, 1, 3, 2).reshape(g * 512, n)


B, L, C, H, W, HID = 2, 2, 128, 16, 16, 16384
BLK = 32
FMT = "e4m3"


def silu(v):
    return v / (1.0 + np.exp(-v))


def _dwt(x):
    x1 = x[:, :, 0::2, 0::2] * 0.5
    x2 = x[:, :, 1::2, 0::2] * 0.5
    x3 = x[:, :, 0::2, 1::2] * 0.5
    x4 = x[:, :, 1::2, 1::2] * 0.5
    return np.concatenate([x1 + x2 + x3 + x4,
                           -x1 - x2 + x3 + x4,
                           -x1 + x2 - x3 + x4,
                           x1 - x2 - x3 + x4], axis=1)


def _idwt(y):
    n, c4, hh, wh = y.shape
    co = c4 // 4
    y1 = y[:, 0 * co:1 * co] * 0.5
    y2 = y[:, 1 * co:2 * co] * 0.5
    y3 = y[:, 2 * co:3 * co] * 0.5
    y4 = y[:, 3 * co:4 * co] * 0.5
    a = y1 - y2 - y3 + y4
    b = y1 - y2 + y3 - y4
    c = y1 + y2 - y3 - y4
    d = y1 + y2 + y3 + y4
    r0 = np.stack([a, c], axis=-1).reshape(n, co, hh, 2 * wh)
    r1 = np.stack([b, d], axis=-1).reshape(n, co, hh, 2 * wh)
    return np.stack([r0, r1], axis=-2).reshape(n, co, 2 * hh, 2 * wh)


def setup_inputs():
    f = np.sort(mx_kscale(4 * C)[::BLK])
    s = np.repeat(f[np.round(np.linspace(0, f.size - 1, C // BLK)).astype(int)], BLK)
    s4 = np.tile(s, 4)
    x = bf(np.random.standard_normal((B, L, C, H, W)) * s[:, None, None])
    conv_w = np.random.standard_normal((HID, 4 * C)) / np.sqrt(4 * C) / s4[None, :]
    conv_w_words, conv_w_scales = pack_weight(np.ascontiguousarray(conv_w.T), FMT)
    conv_b = bf(np.random.standard_normal(HID) * 0.3)
    conv_out_w = np.random.standard_normal((4 * C, HID)) * 1.5 / np.sqrt(HID)
    conv_out_w_words, conv_out_w_scales = pack_weight(np.ascontiguousarray(conv_out_w.T), FMT)
    conv_out_b = bf(np.random.standard_normal(4 * C) * 0.3)
    return {"x": x,
            "conv_w_words": conv_w_words,
            "conv_w_scales": conv_w_scales,
            "conv_b": conv_b,
            "conv_out_w_words": conv_out_w_words,
            "conv_out_w_scales": conv_out_w_scales,
            "conv_out_b": conv_out_b}


def reference(x, conv_w_words, conv_w_scales, conv_b, conv_out_w_words, conv_out_w_scales, conv_out_b):
    x = f64(x)
    b, l, c, h, w = x.shape
    pad_h = (2 - h % 2) % 2
    pad_w = (2 - w % 2) % 2
    if pad_h > 0 or pad_w > 0:
        x = np.pad(x, ((0, 0), (0, 0), (0, 0), (0, pad_h), (0, pad_w)))
    hp, wp = x.shape[-2], x.shape[-1]
    xf = x.reshape(b * l, c, hp, wp)
    x_dwt = _dwt(xf)
    n, c4, hh, wh = x_dwt.shape
    xq = mxq(x_dwt, 1, "e4m3").reshape(n, c4, hh * wh)
    feat = (unpack_weight(conv_w_words, conv_w_scales, FMT).T @ xq) + f64(conv_b)[None, :, None]
    feat = silu(feat)
    y = (unpack_weight(conv_out_w_words, conv_out_w_scales, FMT).T @ mxq(feat, 1, "e4m3")) + f64(conv_out_b)[None, :, None]
    rec = _idwt(y.reshape(n, c4, hh, wh))
    out = rec.reshape(b, l, c, hp, wp)
    if pad_h > 0 or pad_w > 0:
        out = out[..., :h, :w]
    return out

@@ -1,0 +1,284 @@
+from contextlib import ExitStack
+
+import concourse.mybir as mybir
+from concourse.masks import make_identity
+
+F32 = mybir.dt.float32
+BF16 = mybir.dt.bfloat16
+I32 = mybir.dt.int32
+U32 = mybir.dt.uint32
+U8 = mybir.dt.uint8
+FP8X4 = mybir.dt.float8_e4m3fn_x4
+ALU = mybir.AluOpType
+ACT = mybir.ActivationFunctionType
+
+P = 128
+PACK = 4
+K_PASS = P * PACK
+IMAGES = 4
+CHANNELS = 128
+HALF = 8
+PIXELS = HALF * HALF
+TOKENS = IMAGES * PIXELS
+TOKEN_TILES = TOKENS // P
+HIDDEN = 16384
+GROUPS = HIDDEN // K_PASS
+SUBBANDS = 4
+CHUNK = 4
+CHUNKS = GROUPS // CHUNK
+LAG = 6
+
+FLOPS = 2 * 2 * TOKENS * K_PASS * HIDDEN
+
+
+def tile_waveletblock_k_kernel(
+    tc, x, conv_w_words, conv_w_scales, conv_b, conv_out_w_words, conv_out_w_scales, conv_out_b, out
+):
+    nc = tc.nc
+    with ExitStack() as ctx:
+        keep = ctx.enter_context(tc.tile_pool(name="keep", bufs=1))
+        dwt = ctx.enter_context(tc.tile_pool(name="dwt", bufs=2))
+        stages = ctx.enter_context(tc.tile_pool(name="stages", bufs=2 * TOKEN_TILES))
+        groupeds = ctx.enter_context(tc.tile_pool(name="groupeds", bufs=3))
+        quantised = ctx.enter_context(tc.tile_pool(name="quantised", bufs=LAG))
+        psum_first = ctx.enter_context(tc.psum_pool(name="psum_first", bufs=TOKEN_TILES))
+        psum_flip = ctx.enter_context(tc.psum_pool(name="psum_flip", bufs=TOKEN_TILES))
+        psum_wide = ctx.enter_context(tc.psum_pool(name="psum_wide", bufs=SUBBANDS))
+        ctx.enter_context(tc.manual_schedule())
+
+        ident_bf = keep.tile([P, P], BF16)
+        make_identity(nc, ident_bf[:])
+        ident_f32 = keep.tile([P, P], F32)
+        make_identity(nc, ident_f32[:])
+
+        signs = keep.tile([P, 3], F32)
+        nc.vector.memset(signs[:, 0:1], 1.0)
+        nc.vector.memset(signs[64:128, 0:1], -1.0)
+        nc.vector.memset(signs[:, 1:3], 0.5)
+        nc.vector.memset(signs[64:128, 1:2], -0.5)
+        nc.vector.memset(signs[32:64, 2:3], -0.5)
+        nc.vector.memset(signs[64:96, 2:3], -0.5)
+        table_warm = keep.tile([P, 1], F32)
+        nc.scalar.activation(out=table_warm[:], in_=signs[:, 0:1], func=ACT.Silu)
+
+        bias_rows = keep.tile([P, K_PASS], BF16)
+        out_bias_rows = keep.tile([P, P], BF16)
+        x_rep = keep.tile([P, IMAGES, PACK, 4 * PIXELS], BF16)
+        w1_planes = keep.tile([P, HIDDEN // 4], U8, align_bytes=64)
+        w2_planes = keep.tile([P, CHUNKS, K_PASS], U8, align_bytes=64)
+        nc.vector.memset(bias_rows[:], 0.0)
+        nc.vector.memset(out_bias_rows[:], 0.0)
+        nc.vector.memset(w1_planes[:].bitcast(I32), 0)
+        nc.vector.memset(w2_planes[:].rearrange("p c n -> p (c n)").bitcast(I32), 0)
+
+        nc.sync.dma_start(out=bias_rows[0:GROUPS, :], in_=conv_b.rearrange("(g c) -> g c", c=K_PASS))
+        nc.sync.dma_start(
+            out=out_bias_rows[0:SUBBANDS, :], in_=conv_out_b.rearrange("(s c) -> s c", c=CHANNELS)
+        )
+        x_rows = x.rearrange("b l (q t) h w -> q (b l) (t h w)", t=PACK)
+        for s in range(SUBBANDS):
+            nc.sync.dma_start(
+                out=x_rep[32 * s : 32 * (s + 1)].rearrange("p m t f -> p m (t f)"), in_=x_rows
+            )
+        for quad in range(4):
+            nc.sync.dma_start(
+                out=w1_planes[32 * quad : 32 * quad + 16, :].bitcast(I32),
+                in_=conv_w_scales[0, 4 * quad : 4 * quad + 4, :]
+                .rearrange("r (k c) -> k r c", k=4)
+                .bitcast(I32),
+            )
+        w1_flat = conv_w_words[0].rearrange("p n t -> p (n t)")
+        w1_words = []
+        w2_words = []
+        for c in range(CHUNKS):
+            w1_c = keep.tile([P, CHUNK * K_PASS], U32, name="w1_words%d" % c, align_bytes=64)
+            nc.sync.dma_start(
+                out=w1_c[:].bitcast(I32),
+                in_=w1_flat[:, 4 * CHUNK * K_PASS * c : 4 * CHUNK * K_PASS * (c + 1)].bitcast(I32),
+            )
+            w1_words.append(w1_c)
+            for quad in range(4):
+                nc.sync.dma_start(
+                    out=w2_planes[32 * quad : 32 * quad + 16, c, :].bitcast(I32),
+                    in_=conv_out_w_scales[
+                        CHUNK * c : CHUNK * (c + 1), 4 * quad : 4 * quad + 4, :
+                    ].bitcast(I32),
+                )
+            w2_c = keep.tile([P, CHUNK, K_PASS], U32, name="w2_words%d" % c, align_bytes=64)
+            nc.sync.dma_start(
+                out=w2_c[:].bitcast(I32),
+                in_=conv_out_w_words[CHUNK * c : CHUNK * (c + 1)]
+                .rearrange("g p n t -> p g (n t)")
+                .bitcast(I32),
+            )
+            w2_words.append(w2_c)
+
+        out_bias_flip = psum_wide.tile([P, P], BF16, tag="wide")
+        nc.tensor.transpose(out=out_bias_flip[:], in_=out_bias_rows[:], identity=ident_bf[:])
+        half_out_bias = keep.tile([P, SUBBANDS], F32)
+        nc.vector.tensor_scalar(
+            out=half_out_bias[:], in0=out_bias_flip[:, 0:SUBBANDS], scalar1=0.5, scalar2=None, op0=ALU.mult
+        )
+
+        bias_all = keep.tile([P, HIDDEN], BF16)
+        for pair in range(GROUPS // 2):
+            spread = psum_wide.tile([P, 2 * K_PASS], BF16, tag="wide")
+            for half in range(2):
+                g = 2 * pair + half
+                nc.tensor.matmul(
+                    out=spread[:, K_PASS * half : K_PASS * (half + 1)],
+                    lhsT=ident_bf[:, g : g + 1].to_broadcast([P, P]),
+                    rhs=bias_rows[:],
+                    start=True,
+                    stop=True,
+                )
+            nc.scalar.copy(out=bias_all[:, 2 * K_PASS * pair : 2 * K_PASS * (pair + 1)], in_=spread[:])
+
+        d_grouped = keep.tile([P, IMAGES, PIXELS, PACK], BF16, align_bytes=64)
+        for m in range(IMAGES):
+            rows = x_rep[:, m].rearrange("p t (i r w) -> p r t i w", i=HALF, r=2, w=2 * HALF)
+            vert = dwt.tile([P, PACK, HALF, 2 * HALF], F32)
+            nc.vector.scalar_tensor_tensor(
+                out=vert[:], in0=rows[:, 1], scalar=signs[:, 0:1], in1=rows[:, 0], op0=ALU.mult, op1=ALU.add
+            )
+            right = dwt.tile([P, PACK, PIXELS], F32)
+            nc.vector.tensor_scalar(
+                out=right[:],
+                in0=vert[:].rearrange("p t i (j q) -> p q t (i j)", q=2)[:, 1],
+                scalar1=signs[:, 1:2],
+                scalar2=None,
+                op0=ALU.mult,
+            )
+            nc.vector.scalar_tensor_tensor(
+                out=d_grouped[:, m],
+                in0=vert[:].rearrange("p t i (j q) -> p q (i j) t", q=2)[:, 0],
+                scalar=signs[:, 2:3],
+                in1=right[:].rearrange("p t k -> p k t"),
+                op0=ALU.mult,
+                op1=ALU.add,
+            )
+        d_codes = keep.tile([P, TOKENS], U32, align_bytes=64)
+        d_plane = keep.tile([P, TOKENS], U8, align_bytes=64)
+        nc.vector.quantize_mx(
+            out=d_codes[:].bitcast(FP8X4),
+            scales=d_plane[:],
+            in_=d_grouped[:].rearrange("p m k t -> p (m k t)"),
+        )
+
+        stage_of = {}
+        grouped_of = {}
+        codes_of = {}
+        plane_of = {}
+        y = []
+
+        def first_matmul(g):
+            words = w1_words[g // CHUNK]
+            cols = slice(K_PASS * (g % CHUNK), K_PASS * (g % CHUNK + 1))
+            row0 = 4 * (g // 8)
+            plane_cols = slice(K_PASS * (g % 8), K_PASS * (g % 8 + 1))
+            for tt in range(TOKEN_TILES):
+                toks = slice(P * tt, P * (tt + 1))
+                acc = psum_first.tile([P, K_PASS], F32, tag="first")
+                nc.tensor.matmul_mx(
+                    out=acc[:],
+                    lhsT=d_codes[:, toks].bitcast(FP8X4),
+                    lhsT_scale=d_plane[:, toks],
+                    rhs=words[:, cols].bitcast(FP8X4),
+                    rhs_scale=w1_planes[row0:P, plane_cols],
+                    start=True,
+                    stop=True,
+                )
+                stage = stages.tile([P, PACK, P], F32, tag="stage")
+                nc.vector.tensor_tensor(
+                    out=stage[:].rearrange("p t a -> p a t"),
+                    in0=acc[:].rearrange("p (a t) -> p a t", t=PACK),
+                    in1=bias_all[:, K_PASS * g : K_PASS * (g + 1)].rearrange("p (a t) -> p a t", t=PACK),
+                    op=ALU.add,
+                )
+                stage_of[(g, tt)] = stage
+
+        def flip_and_silu(g):
+            grouped = groupeds.tile([P, TOKEN_TILES, P, PACK], BF16, tag="grouped", align_bytes=64)
+            flips = []
+            for tt in range(TOKEN_TILES):
+                flip = psum_flip.tile([P, PACK, P], F32, tag="flip")
+                for t in range(PACK):
+                    nc.tensor.transpose(out=flip[:, t, :], in_=stage_of[(g, tt)][:, t, :], identity=ident_f32[:])
+                flips.append(flip)
+            for tt in range(TOKEN_TILES):
+                nc.scalar.activation(
+                    out=grouped[:, tt], in_=flips[tt][:].rearrange("p t k -> p k t"), func=ACT.Silu
+                )
+            grouped_of[g] = grouped
+
+        def quantise(g):
+            codes = quantised.tile([P, TOKENS], U32, tag="codes", align_bytes=64)
+            plane = quantised.tile([P, TOKENS], U8, tag="plane", align_bytes=64)
+            nc.vector.quantize_mx(
+                out=codes[:].bitcast(FP8X4),
+                scales=plane[:],
+                in_=grouped_of[g][:].rearrange("p a k t -> p (a k t)"),
+            )
+            codes_of[g] = codes
+            plane_of[g] = plane
+
+        def second_matmul(g):
+            words = w2_words[g // CHUNK]
+            row0 = 4 * (g % CHUNK)
+            for s in range(SUBBANDS):
+                cols = slice(P * s, P * (s + 1))
+                nc.tensor.matmul_mx(
+                    out=y[s][:, 0:TOKENS],
+                    lhsT=words[:, g % CHUNK, cols].bitcast(FP8X4),
+                    lhsT_scale=w2_planes[row0:P, g // CHUNK, cols],
+                    rhs=codes_of[g][:].bitcast(FP8X4),
+                    rhs_scale=plane_of[g][:],
+                    start=(g == 0),
+                    stop=(g == GROUPS - 1),
+                )
+
+        for i in range(GROUPS + LAG):
+            if i == LAG:
+                for s in range(SUBBANDS):
+                    y.append(psum_wide.tile([P, K_PASS], F32, name="y%d" % s, tag="wide"))
+            if i >= LAG:
+                second_matmul(i - LAG)
+            if 2 <= i < GROUPS + 2:
+                quantise(i - 2)
+            if i < GROUPS:
+                first_matmul(i)
+            if 1 <= i < GROUPS + 1:
+                flip_and_silu(i - 1)
+
+        z = keep.tile([P, SUBBANDS, TOKENS], F32)
+        for s in range(SUBBANDS):
+            nc.vector.tensor_scalar(
+                out=z[:, s, :],
+                in0=y[s][:, 0:TOKENS],
+                scalar1=0.5,
+                scalar2=half_out_bias[:, s : s + 1],
+                op0=ALU.mult,
+                op1=ALU.add,
+            )
+        sum14 = keep.tile([P, TOKENS], F32)
+        dif14 = keep.tile([P, TOKENS], F32)
+        sum23 = keep.tile([P, TOKENS], F32)
+        dif23 = keep.tile([P, TOKENS], F32)
+        nc.vector.tensor_tensor(out=sum14[:], in0=z[:, 0, :], in1=z[:, 3, :], op=ALU.add)
+        nc.vector.tensor_tensor(out=sum23[:], in0=z[:, 1, :], in1=z[:, 2, :], op=ALU.add)
+        nc.vector.tensor_tensor(out=dif14[:], in0=z[:, 0, :], in1=z[:, 3, :], op=ALU.subtract)
+        nc.vector.tensor_tensor(out=dif23[:], in0=z[:, 1, :], in1=z[:, 2, :], op=ALU.subtract)
+        rec = keep.tile([P, IMAGES * HALF, 2, HALF, 2], F32)
+        spots = rec[:].rearrange("p mi r j q -> p r q mi j")
+
+        def grid(flat):
+            return flat[:].rearrange("p (mi j) -> p mi j", j=HALF)
+
+        nc.vector.tensor_tensor(out=spots[:, 0, 0], in0=grid(sum14), in1=grid(sum23), op=ALU.subtract)
+        nc.vector.tensor_tensor(out=spots[:, 1, 1], in0=grid(sum14), in1=grid(sum23), op=ALU.add)
+        nc.vector.tensor_tensor(out=spots[:, 1, 0], in0=grid(dif14), in1=grid(dif23), op=ALU.subtract)
+        nc.vector.tensor_tensor(out=spots[:, 0, 1], in0=grid(dif14), in1=grid(dif23), op=ALU.add)
+        nc.sync.dma_start(
+            out=out.rearrange("b l c h w -> c (b l) (h w)"),
+            in_=rec[:].rearrange("p (m i) r j q -> p m (i r j q)", m=IMAGES),
+        )

@@ -120,6 +120,8 @@ def tile_waveletblock_k_kernel(
             out=half_out_bias[:], in0=out_bias_flip[:, 0:SUBBANDS], scalar1=0.5, scalar2=None, op0=ALU.mult
         )
 
+        bias_sorted = keep.tile([P, PACK, P], BF16)
+        nc.vector.tensor_copy(out=bias_sorted[:], in_=bias_rows[:].rearrange("p (a t) -> p t a", t=PACK))
         bias_all = keep.tile([P, HIDDEN], BF16)
         for pair in range(GROUPS // 2):
             spread = psum_wide.tile([P, 2 * K_PASS], BF16, tag="wide")
@@ -128,7 +130,7 @@ def tile_waveletblock_k_kernel(
                 nc.tensor.matmul(
                     out=spread[:, K_PASS * half : K_PASS * (half + 1)],
                     lhsT=ident_bf[:, g : g + 1].to_broadcast([P, P]),
-                    rhs=bias_rows[:],
+                    rhs=bias_sorted[:].rearrange("p t a -> p (t a)"),
                     start=True,
                     stop=True,
                 )
@@ -190,9 +192,9 @@ def tile_waveletblock_k_kernel(
                 )
                 stage = stages.tile([P, PACK, P], F32, tag="stage")
                 nc.vector.tensor_tensor(
-                    out=stage[:].rearrange("p t a -> p a t"),
-                    in0=acc[:].rearrange("p (a t) -> p a t", t=PACK),
-                    in1=bias_all[:, K_PASS * g : K_PASS * (g + 1)].rearrange("p (a t) -> p a t", t=PACK),
+                    out=stage[:],
+                    in0=acc[:].rearrange("p (a t) -> p t a", t=PACK),
+                    in1=bias_all[:, K_PASS * g : K_PASS * (g + 1)].rearrange("p (t a) -> p t a", t=PACK),
                     op=ALU.add,
                 )
                 stage_of[(g, tt)] = stage

@@ -39,7 +39,7 @@ def tile_waveletblock_k_kernel(
         keep = ctx.enter_context(tc.tile_pool(name="keep", bufs=1))
         dwt = ctx.enter_context(tc.tile_pool(name="dwt", bufs=2))
         stages = ctx.enter_context(tc.tile_pool(name="stages", bufs=2 * TOKEN_TILES))
-        groupeds = ctx.enter_context(tc.tile_pool(name="groupeds", bufs=3))
+        groupeds = ctx.enter_context(tc.tile_pool(name="groupeds", bufs=4))
         quantised = ctx.enter_context(tc.tile_pool(name="quantised", bufs=LAG))
         psum_first = ctx.enter_context(tc.psum_pool(name="psum_first", bufs=TOKEN_TILES))
         psum_flip = ctx.enter_context(tc.psum_pool(name="psum_flip", bufs=TOKEN_TILES))
@@ -173,31 +173,30 @@ def tile_waveletblock_k_kernel(
         plane_of = {}
         y = []
 
-        def first_matmul(g):
+        def first_matmul(g, tt):
             words = w1_words[g // CHUNK]
             cols = slice(K_PASS * (g % CHUNK), K_PASS * (g % CHUNK + 1))
             row0 = 4 * (g // 8)
             plane_cols = slice(K_PASS * (g % 8), K_PASS * (g % 8 + 1))
-            for tt in range(TOKEN_TILES):
-                toks = slice(P * tt, P * (tt + 1))
-                acc = psum_first.tile([P, K_PASS], F32, tag="first")
-                nc.tensor.matmul_mx(
-                    out=acc[:],
-                    lhsT=d_codes[:, toks].bitcast(FP8X4),
-                    lhsT_scale=d_plane[:, toks],
-                    rhs=words[:, cols].bitcast(FP8X4),
-                    rhs_scale=w1_planes[row0:P, plane_cols],
-                    start=True,
-                    stop=True,
-                )
-                stage = stages.tile([P, PACK, P], F32, tag="stage")
-                nc.vector.tensor_tensor(
-                    out=stage[:],
-                    in0=acc[:].rearrange("p (a t) -> p t a", t=PACK),
-                    in1=bias_all[:, K_PASS * g : K_PASS * (g + 1)].rearrange("p (t a) -> p t a", t=PACK),
-                    op=ALU.add,
-                )
-                stage_of[(g, tt)] = stage
+            toks = slice(P * tt, P * (tt + 1))
+            acc = psum_first.tile([P, K_PASS], F32, tag="first")
+            nc.tensor.matmul_mx(
+                out=acc[:],
+                lhsT=d_codes[:, toks].bitcast(FP8X4),
+                lhsT_scale=d_plane[:, toks],
+                rhs=words[:, cols].bitcast(FP8X4),
+                rhs_scale=w1_planes[row0:P, plane_cols],
+                start=True,
+                stop=True,
+            )
+            stage = stages.tile([P, PACK, P], F32, tag="stage")
+            nc.vector.tensor_tensor(
+                out=stage[:],
+                in0=acc[:].rearrange("p (a t) -> p t a", t=PACK),
+                in1=bias_all[:, K_PASS * g : K_PASS * (g + 1)].rearrange("p (t a) -> p t a", t=PACK),
+                op=ALU.add,
+            )
+            stage_of[(g, tt)] = stage
 
         def flip_and_silu(g):
             grouped = groupeds.tile([P, TOKEN_TILES, P, PACK], BF16, tag="grouped", align_bytes=64)
@@ -243,17 +242,19 @@ def tile_waveletblock_k_kernel(
             if i == LAG:
                 for s in range(SUBBANDS):
                     y.append(psum_wide.tile([P, K_PASS], F32, name="y%d" % s, tag="wide"))
+            if i < GROUPS:
+                first_matmul(i, 0)
             if i >= LAG:
                 second_matmul(i - LAG)
-            if 2 <= i < GROUPS + 2:
-                quantise(i - 2)
             if i < GROUPS:
-                first_matmul(i)
+                first_matmul(i, 1)
+            if 3 <= i < GROUPS + 3:
+                quantise(i - 3)
             if 1 <= i < GROUPS + 1:
                 flip_and_silu(i - 1)
 
         z = keep.tile([P, SUBBANDS, TOKENS], F32)
-        for s in range(SUBBANDS):
+        for s in range(2):
             nc.vector.tensor_scalar(
                 out=z[:, s, :],
                 in0=y[s][:, 0:TOKENS],
@@ -262,25 +263,28 @@ def tile_waveletblock_k_kernel(
                 op0=ALU.mult,
                 op1=ALU.add,
             )
-        sum14 = keep.tile([P, TOKENS], F32)
-        dif14 = keep.tile([P, TOKENS], F32)
-        sum23 = keep.tile([P, TOKENS], F32)
-        dif23 = keep.tile([P, TOKENS], F32)
-        nc.vector.tensor_tensor(out=sum14[:], in0=z[:, 0, :], in1=z[:, 3, :], op=ALU.add)
-        nc.vector.tensor_tensor(out=sum23[:], in0=z[:, 1, :], in1=z[:, 2, :], op=ALU.add)
-        nc.vector.tensor_tensor(out=dif14[:], in0=z[:, 0, :], in1=z[:, 3, :], op=ALU.subtract)
-        nc.vector.tensor_tensor(out=dif23[:], in0=z[:, 1, :], in1=z[:, 2, :], op=ALU.subtract)
-        rec = keep.tile([P, IMAGES * HALF, 2, HALF, 2], F32)
-        spots = rec[:].rearrange("p mi r j q -> p r q mi j")
-
-        def grid(flat):
-            return flat[:].rearrange("p (mi j) -> p mi j", j=HALF)
-
-        nc.vector.tensor_tensor(out=spots[:, 0, 0], in0=grid(sum14), in1=grid(sum23), op=ALU.subtract)
-        nc.vector.tensor_tensor(out=spots[:, 1, 1], in0=grid(sum14), in1=grid(sum23), op=ALU.add)
-        nc.vector.tensor_tensor(out=spots[:, 1, 0], in0=grid(dif14), in1=grid(dif23), op=ALU.subtract)
-        nc.vector.tensor_tensor(out=spots[:, 0, 1], in0=grid(dif14), in1=grid(dif23), op=ALU.add)
+            nc.scalar.activation(
+                out=z[:, 2 + s, :],
+                in_=y[2 + s][:, 0:TOKENS],
+                func=ACT.Identity,
+                bias=half_out_bias[:, 2 + s : 3 + s],
+                scale=0.5,
+            )
+        first = keep.tile([P, 2, 2, TOKENS], F32)
+        nc.vector.tensor_tensor(out=first[:, 0], in0=z[:, 0:2, :], in1=z[:, 2:4, :], op=ALU.subtract)
+        nc.vector.tensor_tensor(out=first[:, 1], in0=z[:, 0:2, :], in1=z[:, 2:4, :], op=ALU.add)
+        planar = keep.tile([P, IMAGES * HALF, 2, 2, HALF], F32)
+        left = first[:, :, 0, :].rearrange("p r (mi j) -> p r mi j", j=HALF)
+        right_half = first[:, :, 1, :].rearrange("p r (mi j) -> p r mi j", j=HALF)
+        by_column = planar[:].rearrange("p mi r q j -> p q r mi j")
+        nc.vector.tensor_tensor(out=by_column[:, 0], in0=left, in1=right_half, op=ALU.subtract)
+        nc.vector.tensor_tensor(out=by_column[:, 1], in0=left, in1=right_half, op=ALU.add)
+        rec = keep.tile([P, IMAGES * HALF * 2, HALF, 2], F32)
+        woven = planar[:].rearrange("p mi r q j -> p (mi r) j q")
+        rows_half = IMAGES * HALF
+        nc.vector.tensor_copy(out=rec[:, 0:rows_half], in_=woven[:, 0:rows_half])
+        nc.scalar.copy(out=rec[:, rows_half : 2 * rows_half], in_=woven[:, rows_half : 2 * rows_half])
         nc.sync.dma_start(
             out=out.rearrange("b l c h w -> c (b l) (h w)"),
-            in_=rec[:].rearrange("p (m i) r j q -> p m (i r j q)", m=IMAGES),
+            in_=rec[:].rearrange("p (m h) j q -> p m (h j q)", m=IMAGES),
         )

@@ -27,6 +27,7 @@ SUBBANDS = 4
 CHUNK = 4
 CHUNKS = GROUPS // CHUNK
 LAG = 6
+SPREAD_BY_TENSOR = GROUPS // 2
 
 FLOPS = 2 * 2 * TOKENS * K_PASS * HIDDEN
 
@@ -37,7 +38,7 @@ def tile_waveletblock_k_kernel(
     nc = tc.nc
     with ExitStack() as ctx:
         keep = ctx.enter_context(tc.tile_pool(name="keep", bufs=1))
-        dwt = ctx.enter_context(tc.tile_pool(name="dwt", bufs=2))
+        dwt = ctx.enter_context(tc.tile_pool(name="dwt", bufs=1))
         stages = ctx.enter_context(tc.tile_pool(name="stages", bufs=2 * TOKEN_TILES))
         groupeds = ctx.enter_context(tc.tile_pool(name="groupeds", bufs=4))
         quantised = ctx.enter_context(tc.tile_pool(name="quantised", bufs=LAG))
@@ -66,7 +67,8 @@ def tile_waveletblock_k_kernel(
         x_rep = keep.tile([P, IMAGES, PACK, 4 * PIXELS], BF16)
         w1_planes = keep.tile([P, HIDDEN // 4], U8, align_bytes=64)
         w2_planes = keep.tile([P, CHUNKS, K_PASS], U8, align_bytes=64)
-        nc.vector.memset(bias_rows[:], 0.0)
+        nc.vector.memset(bias_rows[32:64, :], 0.0)
+        nc.vector.memset(bias_rows[64:128, :], 0.0)
         nc.vector.memset(out_bias_rows[:], 0.0)
         nc.vector.memset(w1_planes[:].bitcast(I32), 0)
         nc.vector.memset(w2_planes[:].rearrange("p c n -> p (c n)").bitcast(I32), 0)
@@ -76,10 +78,12 @@ def tile_waveletblock_k_kernel(
             out=out_bias_rows[0:SUBBANDS, :], in_=conv_out_b.rearrange("(s c) -> s c", c=CHANNELS)
         )
         x_rows = x.rearrange("b l (q t) h w -> q (b l) (t h w)", t=PACK)
-        for s in range(SUBBANDS):
-            nc.sync.dma_start(
-                out=x_rep[32 * s : 32 * (s + 1)].rearrange("p m t f -> p m (t f)"), in_=x_rows
-            )
+        for tt in range(TOKEN_TILES):
+            for s in range(SUBBANDS):
+                nc.sync.dma_start(
+                    out=x_rep[32 * s : 32 * (s + 1), 2 * tt : 2 * tt + 2].rearrange("p m t f -> p m (t f)"),
+                    in_=x_rows[:, 2 * tt : 2 * tt + 2, :],
+                )
         for quad in range(4):
             nc.sync.dma_start(
                 out=w1_planes[32 * quad : 32 * quad + 16, :].bitcast(I32),
@@ -87,6 +91,7 @@ def tile_waveletblock_k_kernel(
                 .rearrange("r (k c) -> k r c", k=4)
                 .bitcast(I32),
             )
+        bias_all = keep.tile([P, HIDDEN], BF16)
         w1_flat = conv_w_words[0].rearrange("p n t -> p (n t)")
         w1_words = []
         w2_words = []
@@ -97,6 +102,9 @@ def tile_waveletblock_k_kernel(
                 in_=w1_flat[:, 4 * CHUNK * K_PASS * c : 4 * CHUNK * K_PASS * (c + 1)].bitcast(I32),
             )
             w1_words.append(w1_c)
+            if CHUNK * c >= SPREAD_BY_TENSOR:
+                hidden = slice(CHUNK * K_PASS * c, CHUNK * K_PASS * (c + 1))
+                nc.sync.dma_start(out=bias_all[:, hidden], in_=conv_b[hidden].partition_broadcast(P))
             for quad in range(4):
                 nc.sync.dma_start(
                     out=w2_planes[32 * quad : 32 * quad + 16, c, :].bitcast(I32),
@@ -113,58 +121,59 @@ def tile_waveletblock_k_kernel(
             )
             w2_words.append(w2_c)
 
-        out_bias_flip = psum_wide.tile([P, P], BF16, tag="wide")
-        nc.tensor.transpose(out=out_bias_flip[:], in_=out_bias_rows[:], identity=ident_bf[:])
-        half_out_bias = keep.tile([P, SUBBANDS], F32)
-        nc.vector.tensor_scalar(
-            out=half_out_bias[:], in0=out_bias_flip[:, 0:SUBBANDS], scalar1=0.5, scalar2=None, op0=ALU.mult
-        )
-
-        bias_sorted = keep.tile([P, PACK, P], BF16)
-        nc.vector.tensor_copy(out=bias_sorted[:], in_=bias_rows[:].rearrange("p (a t) -> p t a", t=PACK))
-        bias_all = keep.tile([P, HIDDEN], BF16)
-        for pair in range(GROUPS // 2):
+        for pair in range(SPREAD_BY_TENSOR // 2):
             spread = psum_wide.tile([P, 2 * K_PASS], BF16, tag="wide")
             for half in range(2):
                 g = 2 * pair + half
                 nc.tensor.matmul(
                     out=spread[:, K_PASS * half : K_PASS * (half + 1)],
                     lhsT=ident_bf[:, g : g + 1].to_broadcast([P, P]),
-                    rhs=bias_sorted[:].rearrange("p t a -> p (t a)"),
+                    rhs=bias_rows[:],
                     start=True,
                     stop=True,
                 )
             nc.scalar.copy(out=bias_all[:, 2 * K_PASS * pair : 2 * K_PASS * (pair + 1)], in_=spread[:])
 
         d_grouped = keep.tile([P, IMAGES, PIXELS, PACK], BF16, align_bytes=64)
-        for m in range(IMAGES):
-            rows = x_rep[:, m].rearrange("p t (i r w) -> p r t i w", i=HALF, r=2, w=2 * HALF)
-            vert = dwt.tile([P, PACK, HALF, 2 * HALF], F32)
+        d_codes = keep.tile([P, TOKENS], U32, align_bytes=64)
+        d_plane = keep.tile([P, TOKENS], U8, align_bytes=64)
+        for tt in range(TOKEN_TILES):
+            rows = x_rep[:, 2 * tt : 2 * tt + 2].rearrange(
+                "p m t (i r w) -> p r m t i w", i=HALF, r=2, w=2 * HALF
+            )
+            vert = dwt.tile([P, 2, PACK, HALF, 2 * HALF], F32)
             nc.vector.scalar_tensor_tensor(
                 out=vert[:], in0=rows[:, 1], scalar=signs[:, 0:1], in1=rows[:, 0], op0=ALU.mult, op1=ALU.add
             )
-            right = dwt.tile([P, PACK, PIXELS], F32)
+            right = dwt.tile([P, 2, PACK, PIXELS], F32)
             nc.vector.tensor_scalar(
                 out=right[:],
-                in0=vert[:].rearrange("p t i (j q) -> p q t (i j)", q=2)[:, 1],
+                in0=vert[:].rearrange("p m t i (j q) -> p q m t (i j)", q=2)[:, 1],
                 scalar1=signs[:, 1:2],
                 scalar2=None,
                 op0=ALU.mult,
             )
-            nc.vector.scalar_tensor_tensor(
-                out=d_grouped[:, m],
-                in0=vert[:].rearrange("p t i (j q) -> p q (i j) t", q=2)[:, 0],
-                scalar=signs[:, 2:3],
-                in1=right[:].rearrange("p t k -> p k t"),
-                op0=ALU.mult,
-                op1=ALU.add,
+            for m in range(2):
+                nc.vector.scalar_tensor_tensor(
+                    out=d_grouped[:, 2 * tt + m],
+                    in0=vert[:, m].rearrange("p t i (j q) -> p q (i j) t", q=2)[:, 0],
+                    scalar=signs[:, 2:3],
+                    in1=right[:, m].rearrange("p t k -> p k t"),
+                    op0=ALU.mult,
+                    op1=ALU.add,
+                )
+            toks = slice(P * tt, P * (tt + 1))
+            nc.vector.quantize_mx(
+                out=d_codes[:, toks].bitcast(FP8X4),
+                scales=d_plane[:, toks],
+                in_=d_grouped[:, 2 * tt : 2 * tt + 2].rearrange("p m k t -> p (m k t)"),
             )
-        d_codes = keep.tile([P, TOKENS], U32, align_bytes=64)
-        d_plane = keep.tile([P, TOKENS], U8, align_bytes=64)
-        nc.vector.quantize_mx(
-            out=d_codes[:].bitcast(FP8X4),
-            scales=d_plane[:],
-            in_=d_grouped[:].rearrange("p m k t -> p (m k t)"),
+
+        out_bias_flip = psum_wide.tile([P, P], BF16, tag="wide")
+        nc.tensor.transpose(out=out_bias_flip[:], in_=out_bias_rows[:], identity=ident_bf[:])
+        half_out_bias = keep.tile([P, SUBBANDS], F32)
+        nc.vector.tensor_scalar(
+            out=half_out_bias[:], in0=out_bias_flip[:, 0:SUBBANDS], scalar1=0.5, scalar2=None, op0=ALU.mult
         )
 
         stage_of = {}
@@ -193,7 +202,7 @@ def tile_waveletblock_k_kernel(
             nc.vector.tensor_tensor(
                 out=stage[:],
                 in0=acc[:].rearrange("p (a t) -> p t a", t=PACK),
-                in1=bias_all[:, K_PASS * g : K_PASS * (g + 1)].rearrange("p (t a) -> p t a", t=PACK),
+                in1=bias_all[:, K_PASS * g : K_PASS * (g + 1)].rearrange("p (a t) -> p t a", t=PACK),
                 op=ALU.add,
             )
             stage_of[(g, tt)] = stage

@@ -41,10 +41,10 @@ def tile_waveletblock_k_kernel(
         dwt = ctx.enter_context(tc.tile_pool(name="dwt", bufs=1))
         stages = ctx.enter_context(tc.tile_pool(name="stages", bufs=2 * TOKEN_TILES))
         groupeds = ctx.enter_context(tc.tile_pool(name="groupeds", bufs=4))
-        quantised = ctx.enter_context(tc.tile_pool(name="quantised", bufs=LAG))
-        psum_first = ctx.enter_context(tc.psum_pool(name="psum_first", bufs=TOKEN_TILES))
-        psum_flip = ctx.enter_context(tc.psum_pool(name="psum_flip", bufs=TOKEN_TILES))
-        psum_wide = ctx.enter_context(tc.psum_pool(name="psum_wide", bufs=SUBBANDS))
+        quantised = ctx.enter_context(tc.tile_pool(name="quantised", bufs=LAG - 2))
+        psum_first = ctx.enter_context(tc.psum_pool(name="psum_first", bufs=3))
+        psum_flip = ctx.enter_context(tc.psum_pool(name="psum_flip", bufs=3))
+        psum_wide = ctx.enter_context(tc.psum_pool(name="psum_wide", bufs=TOKEN_TILES))
         ctx.enter_context(tc.manual_schedule())
 
         ident_bf = keep.tile([P, P], BF16)
@@ -233,24 +233,23 @@ def tile_waveletblock_k_kernel(
             plane_of[g] = plane
 
         def second_matmul(g):
-            words = w2_words[g // CHUNK]
             row0 = 4 * (g % CHUNK)
-            for s in range(SUBBANDS):
-                cols = slice(P * s, P * (s + 1))
+            for tt in range(TOKEN_TILES):
+                toks = slice(P * tt, P * (tt + 1))
                 nc.tensor.matmul_mx(
-                    out=y[s][:, 0:TOKENS],
-                    lhsT=words[:, g % CHUNK, cols].bitcast(FP8X4),
-                    lhsT_scale=w2_planes[row0:P, g // CHUNK, cols],
-                    rhs=codes_of[g][:].bitcast(FP8X4),
-                    rhs_scale=plane_of[g][:],
+                    out=y[tt][:],
+                    lhsT=codes_of[g][:, toks].bitcast(FP8X4),
+                    lhsT_scale=plane_of[g][:, toks],
+                    rhs=w2_words[g // CHUNK][:, g % CHUNK, :].bitcast(FP8X4),
+                    rhs_scale=w2_planes[row0:P, g // CHUNK, :],
                     start=(g == 0),
                     stop=(g == GROUPS - 1),
                 )
 
         for i in range(GROUPS + LAG):
             if i == LAG:
-                for s in range(SUBBANDS):
-                    y.append(psum_wide.tile([P, K_PASS], F32, name="y%d" % s, tag="wide"))
+                for tt in range(TOKEN_TILES):
+                    y.append(psum_wide.tile([P, K_PASS], F32, name="y%d" % tt, tag="wide"))
             if i < GROUPS:
                 first_matmul(i, 0)
             if i >= LAG:
@@ -262,11 +261,24 @@ def tile_waveletblock_k_kernel(
             if 1 <= i < GROUPS + 1:
                 flip_and_silu(i - 1)
 
+        y_sb = keep.tile([P, TOKEN_TILES, K_PASS], F32)
+        nc.vector.tensor_copy(out=y_sb[:, 0, :], in_=y[0][:])
+        nc.scalar.copy(out=y_sb[:, 1, :], in_=y[1][:])
+        y_flip = []
+        for pair in range(2):
+            y_flip.append(psum_flip.tile([P, 2, TOKENS], F32, name="y_flip%d" % pair, tag="flip"))
+        for tt in range(TOKEN_TILES):
+            for s in range(SUBBANDS):
+                nc.tensor.transpose(
+                    out=y_flip[s // 2][:, s % 2, P * tt : P * (tt + 1)],
+                    in_=y_sb[:, tt, P * s : P * (s + 1)],
+                    identity=ident_f32[:],
+                )
         z = keep.tile([P, SUBBANDS, TOKENS], F32)
         for s in range(2):
             nc.vector.tensor_scalar(
                 out=z[:, s, :],
-                in0=y[s][:, 0:TOKENS],
+                in0=y_flip[0][:, s, :],
                 scalar1=0.5,
                 scalar2=half_out_bias[:, s : s + 1],
                 op0=ALU.mult,
@@ -274,7 +286,7 @@ def tile_waveletblock_k_kernel(
             )
             nc.scalar.activation(
                 out=z[:, 2 + s, :],
-                in_=y[2 + s][:, 0:TOKENS],
+                in_=y_flip[1][:, s, :],
                 func=ACT.Identity,
                 bias=half_out_bias[:, 2 + s : 3 + s],
                 scale=0.5,

@@ -17,17 +17,19 @@ PACK = 4
 K_PASS = P * PACK
 IMAGES = 4
 CHANNELS = 128
+QUADS = CHANNELS // PACK
 HALF = 8
 PIXELS = HALF * HALF
 TOKENS = IMAGES * PIXELS
-TOKEN_TILES = TOKENS // P
 HIDDEN = 16384
 GROUPS = HIDDEN // K_PASS
 SUBBANDS = 4
 CHUNK = 4
 CHUNKS = GROUPS // CHUNK
-LAG = 6
-SPREAD_BY_TENSOR = GROUPS // 2
+PLANES = 4
+PER_PLANE = GROUPS // PLANES
+LAG = 3
+AHEAD = 3
 
 FLOPS = 2 * 2 * TOKENS * K_PASS * HIDDEN
 
@@ -38,247 +40,231 @@ def tile_waveletblock_k_kernel(
     nc = tc.nc
     with ExitStack() as ctx:
         keep = ctx.enter_context(tc.tile_pool(name="keep", bufs=1))
-        dwt = ctx.enter_context(tc.tile_pool(name="dwt", bufs=1))
-        stages = ctx.enter_context(tc.tile_pool(name="stages", bufs=2 * TOKEN_TILES))
-        groupeds = ctx.enter_context(tc.tile_pool(name="groupeds", bufs=4))
-        quantised = ctx.enter_context(tc.tile_pool(name="quantised", bufs=LAG - 2))
-        psum_first = ctx.enter_context(tc.psum_pool(name="psum_first", bufs=3))
-        psum_flip = ctx.enter_context(tc.psum_pool(name="psum_flip", bufs=3))
-        psum_wide = ctx.enter_context(tc.psum_pool(name="psum_wide", bufs=TOKEN_TILES))
+        raws = ctx.enter_context(tc.tile_pool(name="raws", bufs=4))
+        planars = ctx.enter_context(tc.tile_pool(name="planars", bufs=3))
+        groupeds = ctx.enter_context(tc.tile_pool(name="groupeds", bufs=3))
+        quantised = ctx.enter_context(tc.tile_pool(name="quantised", bufs=LAG + 1))
+        psum_first = ctx.enter_context(tc.psum_pool(name="psum_first", bufs=4))
+        psum_second = ctx.enter_context(tc.psum_pool(name="psum_second", bufs=SUBBANDS))
         ctx.enter_context(tc.manual_schedule())
 
-        ident_bf = keep.tile([P, P], BF16)
-        make_identity(nc, ident_bf[:])
-        ident_f32 = keep.tile([P, P], F32)
-        make_identity(nc, ident_f32[:])
+        x_sb = keep.tile([P, PACK * 4 * PIXELS], BF16)
+        bias_rows = keep.tile([P, K_PASS + P], BF16)
+        w1_raw_planes = keep.tile([P, PER_PLANE * K_PASS], U8, align_bytes=64)
+        w2_planes = keep.tile([P, PER_PLANE, K_PASS], U8, align_bytes=64)
+        nc.vector.memset(w1_raw_planes[:].bitcast(I32), 0)
+        nc.gpsimd.memset(bias_rows[:].bitcast(I32), 0)
 
-        signs = keep.tile([P, 3], F32)
-        nc.vector.memset(signs[:, 0:1], 1.0)
-        nc.vector.memset(signs[64:128, 0:1], -1.0)
-        nc.vector.memset(signs[:, 1:3], 0.5)
-        nc.vector.memset(signs[64:128, 1:2], -0.5)
-        nc.vector.memset(signs[32:64, 2:3], -0.5)
-        nc.vector.memset(signs[64:96, 2:3], -0.5)
-        table_warm = keep.tile([P, 1], F32)
-        nc.scalar.activation(out=table_warm[:], in_=signs[:, 0:1], func=ACT.Silu)
+        ident = keep.tile([P, P], BF16)
+        make_identity(nc, ident[:])
+        nc.gpsimd.memset(w2_planes[:].rearrange("p c n -> p (c n)").bitcast(I32), 0)
 
-        bias_rows = keep.tile([P, K_PASS], BF16)
-        out_bias_rows = keep.tile([P, P], BF16)
-        x_rep = keep.tile([P, IMAGES, PACK, 4 * PIXELS], BF16)
-        w1_planes = keep.tile([P, HIDDEN // 4], U8, align_bytes=64)
-        w2_planes = keep.tile([P, CHUNKS, K_PASS], U8, align_bytes=64)
-        nc.vector.memset(bias_rows[32:64, :], 0.0)
-        nc.vector.memset(bias_rows[64:128, :], 0.0)
-        nc.vector.memset(out_bias_rows[:], 0.0)
-        nc.vector.memset(w1_planes[:].bitcast(I32), 0)
-        nc.vector.memset(w2_planes[:].rearrange("p c n -> p (c n)").bitcast(I32), 0)
+        nc.sync.dma_start(out=x_sb[:], in_=x.rearrange("b l (q t) h w -> (b l q) (t h w)", t=PACK))
+        w1_flat = conv_w_words[0].rearrange("p n t -> p (n t)")
+        w1_raw = []
+        w2_words = []
 
-        nc.sync.dma_start(out=bias_rows[0:GROUPS, :], in_=conv_b.rearrange("(g c) -> g c", c=K_PASS))
-        nc.sync.dma_start(
-            out=out_bias_rows[0:SUBBANDS, :], in_=conv_out_b.rearrange("(s c) -> s c", c=CHANNELS)
-        )
-        x_rows = x.rearrange("b l (q t) h w -> q (b l) (t h w)", t=PACK)
-        for tt in range(TOKEN_TILES):
-            for s in range(SUBBANDS):
-                nc.sync.dma_start(
-                    out=x_rep[32 * s : 32 * (s + 1), 2 * tt : 2 * tt + 2].rearrange("p m t f -> p m (t f)"),
-                    in_=x_rows[:, 2 * tt : 2 * tt + 2, :],
-                )
+        def load_w1(c, first, count):
+            lo = CHUNK * c + first
+            nc.sync.dma_start(
+                out=w1_raw[c][:, K_PASS * first : K_PASS * (first + count)].bitcast(I32),
+                in_=w1_flat[:, 4 * K_PASS * lo : 4 * K_PASS * (lo + count)].bitcast(I32),
+            )
+
+        for c in range(CHUNKS):
+            w2_c = keep.tile([P, CHUNK, K_PASS], U32, name="w2_words%d" % c, align_bytes=64)
+            w2_words.append(w2_c)
+        w1_raw.append(raws.tile([P, CHUNK * K_PASS], U32, name="w1_raw0", tag="w1_raw", align_bytes=64))
+        load_w1(0, 0, 1)
         for quad in range(4):
             nc.sync.dma_start(
-                out=w1_planes[32 * quad : 32 * quad + 16, :].bitcast(I32),
+                out=w1_raw_planes[32 * quad : 32 * quad + 16, :].bitcast(I32),
                 in_=conv_w_scales[0, 4 * quad : 4 * quad + 4, :]
-                .rearrange("r (k c) -> k r c", k=4)
+                .rearrange("r (k c) -> k r c", k=PLANES)
                 .bitcast(I32),
             )
-        bias_all = keep.tile([P, HIDDEN], BF16)
-        w1_flat = conv_w_words[0].rearrange("p n t -> p (n t)")
-        w1_words = []
-        w2_words = []
-        for c in range(CHUNKS):
-            w1_c = keep.tile([P, CHUNK * K_PASS], U32, name="w1_words%d" % c, align_bytes=64)
-            nc.sync.dma_start(
-                out=w1_c[:].bitcast(I32),
-                in_=w1_flat[:, 4 * CHUNK * K_PASS * c : 4 * CHUNK * K_PASS * (c + 1)].bitcast(I32),
-            )
-            w1_words.append(w1_c)
-            if CHUNK * c >= SPREAD_BY_TENSOR:
-                hidden = slice(CHUNK * K_PASS * c, CHUNK * K_PASS * (c + 1))
-                nc.sync.dma_start(out=bias_all[:, hidden], in_=conv_b[hidden].partition_broadcast(P))
+        nc.sync.dma_start(out=bias_rows[0:GROUPS, 0:K_PASS], in_=conv_b.rearrange("(g c) -> g c", c=K_PASS))
+        nc.sync.dma_start(
+            out=bias_rows[0:SUBBANDS, K_PASS : K_PASS + P], in_=conv_out_b.rearrange("(s c) -> s c", c=CHANNELS)
+        )
+        load_w1(0, 1, CHUNK - 1)
+        for k in range(PLANES):
             for quad in range(4):
                 nc.sync.dma_start(
-                    out=w2_planes[32 * quad : 32 * quad + 16, c, :].bitcast(I32),
-                    in_=conv_out_w_scales[
-                        CHUNK * c : CHUNK * (c + 1), 4 * quad : 4 * quad + 4, :
-                    ].bitcast(I32),
+                    out=w2_planes[32 * quad + 4 * k : 32 * quad + 4 * k + 4, :, :].bitcast(I32),
+                    in_=conv_out_w_scales[PER_PLANE * k : PER_PLANE * (k + 1), 4 * quad : 4 * quad + 4, :]
+                    .rearrange("g r n -> r g n")
+                    .bitcast(I32),
                 )
-            w2_c = keep.tile([P, CHUNK, K_PASS], U32, name="w2_words%d" % c, align_bytes=64)
+        for c in range(CHUNKS):
+            if c > 0:
+                w1_raw.append(raws.tile([P, CHUNK * K_PASS], U32, name="w1_raw%d" % c, tag="w1_raw", align_bytes=64))
+                load_w1(c, 0, CHUNK)
             nc.sync.dma_start(
-                out=w2_c[:].bitcast(I32),
+                out=w2_words[c][:].bitcast(I32),
                 in_=conv_out_w_words[CHUNK * c : CHUNK * (c + 1)]
                 .rearrange("g p n t -> p g (n t)")
                 .bitcast(I32),
             )
-            w2_words.append(w2_c)
 
-        for pair in range(SPREAD_BY_TENSOR // 2):
-            spread = psum_wide.tile([P, 2 * K_PASS], BF16, tag="wide")
-            for half in range(2):
-                g = 2 * pair + half
-                nc.tensor.matmul(
-                    out=spread[:, K_PASS * half : K_PASS * (half + 1)],
-                    lhsT=ident_bf[:, g : g + 1].to_broadcast([P, P]),
-                    rhs=bias_rows[:],
-                    start=True,
-                    stop=True,
-                )
-            nc.scalar.copy(out=bias_all[:, 2 * K_PASS * pair : 2 * K_PASS * (pair + 1)], in_=spread[:])
+        signs = keep.tile([P, 4, SUBBANDS, QUADS], BF16)
+        haar = keep.tile([P, IMAGES, 4, P], BF16)
+        nc.vector.memset(haar[:].rearrange("p m r c -> p (m r c)").bitcast(I32), 0)
+        nc.vector.memset(signs[:], 0.5)
+        nc.vector.memset(signs[:, 0:2, 1, :], -0.5)
+        nc.vector.memset(signs[:, 0:3:2, 2, :], -0.5)
+        nc.vector.memset(signs[:, 1:3, 3, :], -0.5)
+        for m in range(IMAGES):
+            rows = slice(QUADS * m, QUADS * (m + 1))
+            nc.vector.tensor_tensor(
+                out=haar[rows, m].rearrange("p r (s q) -> p (r s) q", q=QUADS),
+                in0=signs[rows].rearrange("p r s q -> p (r s) q"),
+                in1=ident[rows, rows].unsqueeze(1).to_broadcast([QUADS, 4 * SUBBANDS, QUADS]),
+                op=ALU.mult,
+            )
+        table_warm = keep.tile([P, 1], F32)
+        nc.scalar.activation(out=table_warm[:], in_=signs[:, 0, 0, 0:1], func=ACT.Silu)
 
         d_grouped = keep.tile([P, IMAGES, PIXELS, PACK], BF16, align_bytes=64)
         d_codes = keep.tile([P, TOKENS], U32, align_bytes=64)
         d_plane = keep.tile([P, TOKENS], U8, align_bytes=64)
-        for tt in range(TOKEN_TILES):
-            rows = x_rep[:, 2 * tt : 2 * tt + 2].rearrange(
-                "p m t (i r w) -> p r m t i w", i=HALF, r=2, w=2 * HALF
+        x_par = x_sb[:].rearrange("p (t i a j b) -> p a b t i j", t=PACK, i=HALF, a=2, j=HALF, b=2)
+        for pair in range(2):
+            d_acc = psum_second.tile([P, 2, PACK * PIXELS], F32, name="d_acc%d" % pair, tag="second")
+            for half in range(2):
+                for r in range(4):
+                    nc.tensor.matmul(
+                        out=d_acc[:, half, :],
+                        lhsT=haar[:, 2 * pair + half, r, :],
+                        rhs=x_par[:, r % 2, r // 2],
+                        start=(r == 0),
+                        stop=(r == 3),
+                    )
+            nc.scalar.copy(
+                out=d_grouped[:, 2 * pair : 2 * pair + 2],
+                in_=d_acc[:].rearrange("p m (t k) -> p m k t", t=PACK),
             )
-            vert = dwt.tile([P, 2, PACK, HALF, 2 * HALF], F32)
-            nc.vector.scalar_tensor_tensor(
-                out=vert[:], in0=rows[:, 1], scalar=signs[:, 0:1], in1=rows[:, 0], op0=ALU.mult, op1=ALU.add
-            )
-            right = dwt.tile([P, 2, PACK, PIXELS], F32)
-            nc.vector.tensor_scalar(
-                out=right[:],
-                in0=vert[:].rearrange("p m t i (j q) -> p q m t (i j)", q=2)[:, 1],
-                scalar1=signs[:, 1:2],
-                scalar2=None,
-                op0=ALU.mult,
-            )
-            for m in range(2):
-                nc.vector.scalar_tensor_tensor(
-                    out=d_grouped[:, 2 * tt + m],
-                    in0=vert[:, m].rearrange("p t i (j q) -> p q (i j) t", q=2)[:, 0],
-                    scalar=signs[:, 2:3],
-                    in1=right[:, m].rearrange("p t k -> p k t"),
-                    op0=ALU.mult,
-                    op1=ALU.add,
-                )
-            toks = slice(P * tt, P * (tt + 1))
-            nc.vector.quantize_mx(
-                out=d_codes[:, toks].bitcast(FP8X4),
-                scales=d_plane[:, toks],
-                in_=d_grouped[:, 2 * tt : 2 * tt + 2].rearrange("p m k t -> p (m k t)"),
-            )
-
-        out_bias_flip = psum_wide.tile([P, P], BF16, tag="wide")
-        nc.tensor.transpose(out=out_bias_flip[:], in_=out_bias_rows[:], identity=ident_bf[:])
-        half_out_bias = keep.tile([P, SUBBANDS], F32)
-        nc.vector.tensor_scalar(
-            out=half_out_bias[:], in0=out_bias_flip[:, 0:SUBBANDS], scalar1=0.5, scalar2=None, op0=ALU.mult
+        nc.vector.quantize_mx(
+            out=d_codes[:].bitcast(FP8X4),
+            scales=d_plane[:],
+            in_=d_grouped[:].rearrange("p m k t -> p (m k t)"),
         )
 
-        stage_of = {}
-        grouped_of = {}
+        bias_flip = psum_second.tile([P, PACK + 1, P], BF16, name="bias_flip", tag="second")
+        for t in range(PACK):
+            nc.tensor.transpose(
+                out=bias_flip[:, t, :],
+                in_=bias_rows[:, 0:K_PASS].rearrange("g (p t) -> g t p", t=PACK)[:, t],
+                identity=ident[:],
+            )
+        nc.tensor.transpose(out=bias_flip[:, PACK, :], in_=bias_rows[:, K_PASS : K_PASS + P], identity=ident[:])
+        bias = keep.tile([P, PACK, GROUPS], F32)
+        half_out_bias = keep.tile([P, SUBBANDS], F32)
+        nc.scalar.copy(out=bias[:], in_=bias_flip[:, 0:PACK, 0:GROUPS])
+        nc.scalar.mul(half_out_bias[:], bias_flip[:, PACK, 0:SUBBANDS], 0.5)
+
+        w1_sorted = keep.tile([P, GROUPS, K_PASS], U32, align_bytes=64)
+        w1_planes = keep.tile([P, PER_PLANE * K_PASS], U8, align_bytes=64)
+        planar_of = {}
         codes_of = {}
         plane_of = {}
         y = []
 
-        def first_matmul(g, tt):
-            words = w1_words[g // CHUNK]
-            cols = slice(K_PASS * (g % CHUNK), K_PASS * (g % CHUNK + 1))
-            row0 = 4 * (g // 8)
-            plane_cols = slice(K_PASS * (g % 8), K_PASS * (g % 8 + 1))
-            toks = slice(P * tt, P * (tt + 1))
-            acc = psum_first.tile([P, K_PASS], F32, tag="first")
-            nc.tensor.matmul_mx(
-                out=acc[:],
-                lhsT=d_codes[:, toks].bitcast(FP8X4),
-                lhsT_scale=d_plane[:, toks],
-                rhs=words[:, cols].bitcast(FP8X4),
-                rhs_scale=w1_planes[row0:P, plane_cols],
-                start=True,
-                stop=True,
+        def sort_words(g):
+            lo = K_PASS * (g % CHUNK)
+            nc.vector.tensor_copy(
+                out=w1_sorted[:, g, :].bitcast(I32).rearrange("p (t m) -> p t m", t=PACK),
+                in_=w1_raw[g // CHUNK][:, lo : lo + K_PASS].bitcast(I32).rearrange("p (m t) -> p t m", t=PACK),
             )
-            stage = stages.tile([P, PACK, P], F32, tag="stage")
-            nc.vector.tensor_tensor(
-                out=stage[:],
-                in0=acc[:].rearrange("p (a t) -> p t a", t=PACK),
-                in1=bias_all[:, K_PASS * g : K_PASS * (g + 1)].rearrange("p (a t) -> p t a", t=PACK),
-                op=ALU.add,
-            )
-            stage_of[(g, tt)] = stage
 
-        def flip_and_silu(g):
-            grouped = groupeds.tile([P, TOKEN_TILES, P, PACK], BF16, tag="grouped", align_bytes=64)
-            flips = []
-            for tt in range(TOKEN_TILES):
-                flip = psum_flip.tile([P, PACK, P], F32, tag="flip")
-                for t in range(PACK):
-                    nc.tensor.transpose(out=flip[:, t, :], in_=stage_of[(g, tt)][:, t, :], identity=ident_f32[:])
-                flips.append(flip)
-            for tt in range(TOKEN_TILES):
-                nc.scalar.activation(
-                    out=grouped[:, tt], in_=flips[tt][:].rearrange("p t k -> p k t"), func=ACT.Silu
+        def sort_planes(piece):
+            cols = slice(K_PASS * piece, K_PASS * (piece + 1))
+            nc.vector.tensor_copy(
+                out=w1_planes[:, cols].rearrange("p (t m) -> p t m", t=PACK),
+                in_=w1_raw_planes[:, cols].rearrange("p (m t) -> p t m", t=PACK),
+            )
+
+        def first_matmul(g, pair):
+            row0 = 4 * (g // PER_PLANE)
+            acc = psum_first.tile([P, 2, TOKENS], F32, tag="first")
+            for half in range(2):
+                t = 2 * pair + half
+                cols = slice(P * t, P * (t + 1))
+                plane_cols = slice(K_PASS * (g % PER_PLANE) + P * t, K_PASS * (g % PER_PLANE) + P * (t + 1))
+                nc.tensor.matmul_mx(
+                    out=acc[:, half, :],
+                    lhsT=w1_sorted[:, g, cols].bitcast(FP8X4),
+                    lhsT_scale=w1_planes[row0:P, plane_cols],
+                    rhs=d_codes[:].bitcast(FP8X4),
+                    rhs_scale=d_plane[:],
+                    start=True,
+                    stop=True,
                 )
-            grouped_of[g] = grouped
+            if pair == 0:
+                planar_of[g] = planars.tile([P, PACK, TOKENS], BF16, name="planar", tag="planar")
+            for half in range(2):
+                t = 2 * pair + half
+                nc.scalar.activation(
+                    out=planar_of[g][:, t, :], in_=acc[:, half, :], func=ACT.Silu, bias=bias[:, t, g : g + 1]
+                )
 
-        def quantise(g):
-            codes = quantised.tile([P, TOKENS], U32, tag="codes", align_bytes=64)
-            plane = quantised.tile([P, TOKENS], U8, tag="plane", align_bytes=64)
+        def interleave(g):
+            grouped = groupeds.tile([P, TOKENS, PACK], BF16, name="grouped", tag="grouped", align_bytes=64)
+            nc.vector.tensor_copy(out=grouped[:], in_=planar_of[g][:].rearrange("p t k -> p k t"))
+            return grouped
+
+        def quantise(g, grouped):
+            codes = quantised.tile([P, TOKENS], U32, name="codes", tag="codes", align_bytes=64)
+            plane = quantised.tile([P, TOKENS], U8, name="plane", tag="plane", align_bytes=64)
             nc.vector.quantize_mx(
-                out=codes[:].bitcast(FP8X4),
-                scales=plane[:],
-                in_=grouped_of[g][:].rearrange("p a k t -> p (a k t)"),
+                out=codes[:].bitcast(FP8X4), scales=plane[:], in_=grouped[:].rearrange("p k t -> p (k t)")
             )
             codes_of[g] = codes
             plane_of[g] = plane
 
-        def second_matmul(g):
-            row0 = 4 * (g % CHUNK)
-            for tt in range(TOKEN_TILES):
-                toks = slice(P * tt, P * (tt + 1))
+        def second_matmul(g, tiles):
+            row0 = 4 * (g // PER_PLANE)
+            for s in tiles:
+                cols = slice(P * s, P * (s + 1))
                 nc.tensor.matmul_mx(
-                    out=y[tt][:],
-                    lhsT=codes_of[g][:, toks].bitcast(FP8X4),
-                    lhsT_scale=plane_of[g][:, toks],
-                    rhs=w2_words[g // CHUNK][:, g % CHUNK, :].bitcast(FP8X4),
-                    rhs_scale=w2_planes[row0:P, g // CHUNK, :],
+                    out=y[s][:],
+                    lhsT=w2_words[g // CHUNK][:, g % CHUNK, cols].bitcast(FP8X4),
+                    lhsT_scale=w2_planes[row0:P, g % PER_PLANE, cols],
+                    rhs=codes_of[g][:].bitcast(FP8X4),
+                    rhs_scale=plane_of[g][:],
                     start=(g == 0),
                     stop=(g == GROUPS - 1),
                 )
 
+        for g in range(AHEAD):
+            sort_planes(g)
+            sort_words(g)
         for i in range(GROUPS + LAG):
             if i == LAG:
-                for tt in range(TOKEN_TILES):
-                    y.append(psum_wide.tile([P, K_PASS], F32, name="y%d" % tt, tag="wide"))
+                for s in range(SUBBANDS):
+                    y.append(psum_second.tile([P, TOKENS], F32, name="y%d" % s, tag="second"))
             if i < GROUPS:
                 first_matmul(i, 0)
             if i >= LAG:
-                second_matmul(i - LAG)
+                second_matmul(i - LAG, (0, 1))
             if i < GROUPS:
                 first_matmul(i, 1)
-            if 3 <= i < GROUPS + 3:
-                quantise(i - 3)
-            if 1 <= i < GROUPS + 1:
-                flip_and_silu(i - 1)
+            if i >= LAG:
+                second_matmul(i - LAG, (2, 3))
+            if 1 <= i <= GROUPS:
+                grouped = interleave(i - 1)
+            if i + AHEAD < PER_PLANE:
+                sort_planes(i + AHEAD)
+            if i + AHEAD < GROUPS:
+                sort_words(i + AHEAD)
+            if 1 <= i <= GROUPS:
+                quantise(i - 1, grouped)
 
-        y_sb = keep.tile([P, TOKEN_TILES, K_PASS], F32)
-        nc.vector.tensor_copy(out=y_sb[:, 0, :], in_=y[0][:])
-        nc.scalar.copy(out=y_sb[:, 1, :], in_=y[1][:])
-        y_flip = []
-        for pair in range(2):
-            y_flip.append(psum_flip.tile([P, 2, TOKENS], F32, name="y_flip%d" % pair, tag="flip"))
-        for tt in range(TOKEN_TILES):
-            for s in range(SUBBANDS):
-                nc.tensor.transpose(
-                    out=y_flip[s // 2][:, s % 2, P * tt : P * (tt + 1)],
-                    in_=y_sb[:, tt, P * s : P * (s + 1)],
-                    identity=ident_f32[:],
-                )
         z = keep.tile([P, SUBBANDS, TOKENS], F32)
         for s in range(2):
             nc.vector.tensor_scalar(
                 out=z[:, s, :],
-                in0=y_flip[0][:, s, :],
+                in0=y[s][:],
                 scalar1=0.5,
                 scalar2=half_out_bias[:, s : s + 1],
                 op0=ALU.mult,
@@ -286,7 +272,7 @@ def tile_waveletblock_k_kernel(
             )
             nc.scalar.activation(
                 out=z[:, 2 + s, :],
-                in_=y_flip[1][:, s, :],
+                in_=y[2 + s][:],
                 func=ACT.Identity,
                 bias=half_out_bias[:, 2 + s : 3 + s],
                 scale=0.5,

@@ -25,11 +25,11 @@ HIDDEN = 16384
 GROUPS = HIDDEN // K_PASS
 SUBBANDS = 4
 CHUNK = 4
-CHUNKS = GROUPS // CHUNK
+LOAD = 2
 PLANES = 4
 PER_PLANE = GROUPS // PLANES
 LAG = 3
-AHEAD = 3
+AHEAD = 2
 
 FLOPS = 2 * 2 * TOKENS * K_PASS * HIDDEN
 
@@ -62,20 +62,24 @@ def tile_waveletblock_k_kernel(
         nc.sync.dma_start(out=x_sb[:], in_=x.rearrange("b l (q t) h w -> (b l q) (t h w)", t=PACK))
         w1_flat = conv_w_words[0].rearrange("p n t -> p (n t)")
         w1_raw = []
-        w2_words = []
+        w2_words = keep.tile([P, GROUPS, K_PASS], U32, align_bytes=64)
 
-        def load_w1(c, first, count):
-            lo = CHUNK * c + first
+        def load_w1(g, count):
+            if g % CHUNK == 0:
+                w1_raw.append(raws.tile([P, CHUNK * K_PASS], U32, name="w1_raw%d" % g, tag="w1_raw", align_bytes=64))
+            first = K_PASS * (g % CHUNK)
             nc.sync.dma_start(
-                out=w1_raw[c][:, K_PASS * first : K_PASS * (first + count)].bitcast(I32),
-                in_=w1_flat[:, 4 * K_PASS * lo : 4 * K_PASS * (lo + count)].bitcast(I32),
+                out=w1_raw[g // CHUNK][:, first : first + K_PASS * count].bitcast(I32),
+                in_=w1_flat[:, 4 * K_PASS * g : 4 * K_PASS * (g + count)].bitcast(I32),
             )
 
-        for c in range(CHUNKS):
-            w2_c = keep.tile([P, CHUNK, K_PASS], U32, name="w2_words%d" % c, align_bytes=64)
-            w2_words.append(w2_c)
-        w1_raw.append(raws.tile([P, CHUNK * K_PASS], U32, name="w1_raw0", tag="w1_raw", align_bytes=64))
-        load_w1(0, 0, 1)
+        def load_w2(g, count):
+            nc.sync.dma_start(
+                out=w2_words[:, g : g + count, :].bitcast(I32),
+                in_=conv_out_w_words[g : g + count].rearrange("g p n t -> p g (n t)").bitcast(I32),
+            )
+
+        load_w1(0, 1)
         for quad in range(4):
             nc.sync.dma_start(
                 out=w1_raw_planes[32 * quad : 32 * quad + 16, :].bitcast(I32),
@@ -87,7 +91,8 @@ def tile_waveletblock_k_kernel(
         nc.sync.dma_start(
             out=bias_rows[0:SUBBANDS, K_PASS : K_PASS + P], in_=conv_out_b.rearrange("(s c) -> s c", c=CHANNELS)
         )
-        load_w1(0, 1, CHUNK - 1)
+        load_w1(1, 1)
+        load_w1(2, 2)
         for k in range(PLANES):
             for quad in range(4):
                 nc.sync.dma_start(
@@ -96,34 +101,46 @@ def tile_waveletblock_k_kernel(
                     .rearrange("g r n -> r g n")
                     .bitcast(I32),
                 )
-        for c in range(CHUNKS):
-            if c > 0:
-                w1_raw.append(raws.tile([P, CHUNK * K_PASS], U32, name="w1_raw%d" % c, tag="w1_raw", align_bytes=64))
-                load_w1(c, 0, CHUNK)
-            nc.sync.dma_start(
-                out=w2_words[c][:].bitcast(I32),
-                in_=conv_out_w_words[CHUNK * c : CHUNK * (c + 1)]
-                .rearrange("g p n t -> p g (n t)")
-                .bitcast(I32),
-            )
+        for g in range(0, GROUPS, LOAD):
+            if g + 4 < GROUPS:
+                load_w1(g + 4, LOAD)
+            load_w2(g, LOAD)
 
         signs = keep.tile([P, 4, SUBBANDS, QUADS], BF16)
         haar = keep.tile([P, IMAGES, 4, P], BF16)
-        nc.vector.memset(haar[:].rearrange("p m r c -> p (m r c)").bitcast(I32), 0)
         nc.vector.memset(signs[:], 0.5)
         nc.vector.memset(signs[:, 0:2, 1, :], -0.5)
         nc.vector.memset(signs[:, 0:3:2, 2, :], -0.5)
         nc.vector.memset(signs[:, 1:3, 3, :], -0.5)
         for m in range(IMAGES):
-            rows = slice(QUADS * m, QUADS * (m + 1))
             nc.vector.tensor_tensor(
-                out=haar[rows, m].rearrange("p r (s q) -> p (r s) q", q=QUADS),
-                in0=signs[rows].rearrange("p r s q -> p (r s) q"),
-                in1=ident[rows, rows].unsqueeze(1).to_broadcast([QUADS, 4 * SUBBANDS, QUADS]),
+                out=haar[:, m].rearrange("p r (s q) -> p (r s) q", q=QUADS),
+                in0=signs[:].rearrange("p r s q -> p (r s) q"),
+                in1=ident[:, QUADS * m : QUADS * (m + 1)].unsqueeze(1).to_broadcast([P, 4 * SUBBANDS, QUADS]),
                 op=ALU.mult,
             )
         table_warm = keep.tile([P, 1], F32)
         nc.scalar.activation(out=table_warm[:], in_=signs[:, 0, 0, 0:1], func=ACT.Silu)
+
+        w1_sorted = keep.tile([P, GROUPS, K_PASS], U32, align_bytes=64)
+        w1_planes = keep.tile([P, PER_PLANE * K_PASS], U8, align_bytes=64)
+
+        def sort_words(g):
+            lo = K_PASS * (g % CHUNK)
+            nc.vector.tensor_copy(
+                out=w1_sorted[:, g, :].bitcast(I32).rearrange("p (t m) -> p m t", t=PACK),
+                in_=w1_raw[g // CHUNK][:, lo : lo + K_PASS].bitcast(I32).rearrange("p (m t) -> p m t", t=PACK),
+            )
+
+        def sort_planes(piece):
+            cols = slice(K_PASS * piece, K_PASS * (piece + 1))
+            nc.vector.tensor_copy(
+                out=w1_planes[:, cols].rearrange("p (t m) -> p t m", t=PACK),
+                in_=w1_raw_planes[:, cols].rearrange("p (m t) -> p t m", t=PACK),
+            )
+
+        sort_words(0)
+        sort_planes(0)
 
         d_grouped = keep.tile([P, IMAGES, PIXELS, PACK], BF16, align_bytes=64)
         d_codes = keep.tile([P, TOKENS], U32, align_bytes=64)
@@ -140,15 +157,18 @@ def tile_waveletblock_k_kernel(
                         start=(r == 0),
                         stop=(r == 3),
                     )
-            nc.scalar.copy(
-                out=d_grouped[:, 2 * pair : 2 * pair + 2],
-                in_=d_acc[:].rearrange("p m (t k) -> p m k t", t=PACK),
+            images = slice(2 * pair, 2 * pair + 2)
+            toks = slice(P * pair, P * (pair + 1))
+            by_token = d_acc[:].rearrange("p m (t k) -> p m k t", t=PACK)
+            if pair == 0:
+                nc.scalar.copy(out=d_grouped[:, images], in_=by_token)
+            else:
+                nc.vector.tensor_copy(out=d_grouped[:, images], in_=by_token)
+            nc.vector.quantize_mx(
+                out=d_codes[:, toks].bitcast(FP8X4),
+                scales=d_plane[:, toks],
+                in_=d_grouped[:, images].rearrange("p m k t -> p (m k t)"),
             )
-        nc.vector.quantize_mx(
-            out=d_codes[:].bitcast(FP8X4),
-            scales=d_plane[:],
-            in_=d_grouped[:].rearrange("p m k t -> p (m k t)"),
-        )
 
         bias_flip = psum_second.tile([P, PACK + 1, P], BF16, name="bias_flip", tag="second")
         for t in range(PACK):
@@ -163,26 +183,10 @@ def tile_waveletblock_k_kernel(
         nc.scalar.copy(out=bias[:], in_=bias_flip[:, 0:PACK, 0:GROUPS])
         nc.scalar.mul(half_out_bias[:], bias_flip[:, PACK, 0:SUBBANDS], 0.5)
 
-        w1_sorted = keep.tile([P, GROUPS, K_PASS], U32, align_bytes=64)
-        w1_planes = keep.tile([P, PER_PLANE * K_PASS], U8, align_bytes=64)
         planar_of = {}
         codes_of = {}
         plane_of = {}
         y = []
-
-        def sort_words(g):
-            lo = K_PASS * (g % CHUNK)
-            nc.vector.tensor_copy(
-                out=w1_sorted[:, g, :].bitcast(I32).rearrange("p (t m) -> p t m", t=PACK),
-                in_=w1_raw[g // CHUNK][:, lo : lo + K_PASS].bitcast(I32).rearrange("p (m t) -> p t m", t=PACK),
-            )
-
-        def sort_planes(piece):
-            cols = slice(K_PASS * piece, K_PASS * (piece + 1))
-            nc.vector.tensor_copy(
-                out=w1_planes[:, cols].rearrange("p (t m) -> p t m", t=PACK),
-                in_=w1_raw_planes[:, cols].rearrange("p (m t) -> p t m", t=PACK),
-            )
 
         def first_matmul(g, pair):
             row0 = 4 * (g // PER_PLANE)
@@ -228,7 +232,7 @@ def tile_waveletblock_k_kernel(
                 cols = slice(P * s, P * (s + 1))
                 nc.tensor.matmul_mx(
                     out=y[s][:],
-                    lhsT=w2_words[g // CHUNK][:, g % CHUNK, cols].bitcast(FP8X4),
+                    lhsT=w2_words[:, g, cols].bitcast(FP8X4),
                     lhsT_scale=w2_planes[row0:P, g % PER_PLANE, cols],
                     rhs=codes_of[g][:].bitcast(FP8X4),
                     rhs_scale=plane_of[g][:],
@@ -236,9 +240,9 @@ def tile_waveletblock_k_kernel(
                     stop=(g == GROUPS - 1),
                 )
 
-        for g in range(AHEAD):
-            sort_planes(g)
+        for g in range(1, AHEAD):
             sort_words(g)
+            sort_planes(g)
         for i in range(GROUPS + LAG):
             if i == LAG:
                 for s in range(SUBBANDS):

@@ -214,7 +214,10 @@ def tile_waveletblock_k_kernel(
 
         def interleave(g):
             grouped = groupeds.tile([P, TOKENS, PACK], BF16, name="grouped", tag="grouped", align_bytes=64)
-            nc.vector.tensor_copy(out=grouped[:], in_=planar_of[g][:].rearrange("p t k -> p k t"))
+            nc.vector.tensor_copy(
+                out=grouped[:].rearrange("p (c i) t -> p c t i", i=4),
+                in_=planar_of[g][:].rearrange("p t (c i) -> p c t i", i=4),
+            )
             return grouped
 
         def quantise(g, grouped):

@@ -28,7 +28,8 @@ CHUNK = 4
 LOAD = 2
 PLANES = 4
 PER_PLANE = GROUPS // PLANES
-LAG = 3
+EARLY = 2
+LAG = 4
 AHEAD = 2
 
 FLOPS = 2 * 2 * TOKENS * K_PASS * HIDDEN
@@ -51,13 +52,16 @@ def tile_waveletblock_k_kernel(
         x_sb = keep.tile([P, PACK * 4 * PIXELS], BF16)
         bias_rows = keep.tile([P, K_PASS + P], BF16)
         w1_raw_planes = keep.tile([P, PER_PLANE * K_PASS], U8, align_bytes=64)
-        w2_planes = keep.tile([P, PER_PLANE, K_PASS], U8, align_bytes=64)
+        w2_planes = [
+            keep.tile([P, PER_PLANE, K_PASS], U8, name="w2_planes%d" % j, align_bytes=64) for j in range(PLANES // 2)
+        ]
         nc.vector.memset(w1_raw_planes[:].bitcast(I32), 0)
         nc.gpsimd.memset(bias_rows[:].bitcast(I32), 0)
 
         ident = keep.tile([P, P], BF16)
         make_identity(nc, ident[:])
-        nc.gpsimd.memset(w2_planes[:].rearrange("p c n -> p (c n)").bitcast(I32), 0)
+        for planes in w2_planes:
+            nc.gpsimd.memset(planes[:].rearrange("p c n -> p (c n)").bitcast(I32), 0)
 
         nc.sync.dma_start(out=x_sb[:], in_=x.rearrange("b l (q t) h w -> (b l q) (t h w)", t=PACK))
         w1_flat = conv_w_words[0].rearrange("p n t -> p (n t)")
@@ -79,32 +83,45 @@ def tile_waveletblock_k_kernel(
                 in_=conv_out_w_words[g : g + count].rearrange("g p n t -> p g (n t)").bitcast(I32),
             )
 
+        def load_w1_planes(first, count):
+            cols = slice(K_PASS * first, K_PASS * (first + count))
+            for quad in range(4):
+                nc.sync.dma_start(
+                    out=w1_raw_planes[32 * quad : 32 * quad + 16, cols].bitcast(I32),
+                    in_=conv_w_scales[0, 4 * quad : 4 * quad + 4, :]
+                    .rearrange("r (k c) -> k r c", k=PLANES)[:, :, cols]
+                    .bitcast(I32),
+                )
+
+        def load_w2_planes(k):
+            row0 = 4 * (k % 2)
+            for quad in range(4):
+                nc.sync.dma_start(
+                    out=w2_planes[k // 2][32 * quad + row0 : 32 * quad + row0 + 4, :, :].bitcast(I32),
+                    in_=conv_out_w_scales[PER_PLANE * k : PER_PLANE * (k + 1), 4 * quad : 4 * quad + 4, :]
+                    .rearrange("g r n -> r g n")
+                    .bitcast(I32),
+                )
+
         load_w1(0, 1)
-        for quad in range(4):
-            nc.sync.dma_start(
-                out=w1_raw_planes[32 * quad : 32 * quad + 16, :].bitcast(I32),
-                in_=conv_w_scales[0, 4 * quad : 4 * quad + 4, :]
-                .rearrange("r (k c) -> k r c", k=PLANES)
-                .bitcast(I32),
-            )
+        load_w1_planes(0, EARLY)
         nc.sync.dma_start(out=bias_rows[0:GROUPS, 0:K_PASS], in_=conv_b.rearrange("(g c) -> g c", c=K_PASS))
         nc.sync.dma_start(
             out=bias_rows[0:SUBBANDS, K_PASS : K_PASS + P], in_=conv_out_b.rearrange("(s c) -> s c", c=CHANNELS)
         )
         load_w1(1, 1)
         load_w1(2, 2)
-        for k in range(PLANES):
-            for quad in range(4):
-                nc.sync.dma_start(
-                    out=w2_planes[32 * quad + 4 * k : 32 * quad + 4 * k + 4, :, :].bitcast(I32),
-                    in_=conv_out_w_scales[PER_PLANE * k : PER_PLANE * (k + 1), 4 * quad : 4 * quad + 4, :]
-                    .rearrange("g r n -> r g n")
-                    .bitcast(I32),
-                )
+        load_w1_planes(EARLY, PER_PLANE - EARLY)
+        load_w1(4, 2)
+        load_w2_planes(0)
+        load_w2_planes(1)
         for g in range(0, GROUPS, LOAD):
-            if g + 4 < GROUPS:
-                load_w1(g + 4, LOAD)
+            if g == PER_PLANE:
+                load_w2_planes(2)
+                load_w2_planes(3)
             load_w2(g, LOAD)
+            if g + 6 < GROUPS:
+                load_w1(g + 6, LOAD)
 
         signs = keep.tile([P, 4, SUBBANDS, QUADS], BF16)
         haar = keep.tile([P, IMAGES, 4, P], BF16)
@@ -230,13 +247,13 @@ def tile_waveletblock_k_kernel(
             plane_of[g] = plane
 
         def second_matmul(g, tiles):
-            row0 = 4 * (g // PER_PLANE)
+            plane = g // PER_PLANE
             for s in tiles:
                 cols = slice(P * s, P * (s + 1))
                 nc.tensor.matmul_mx(
                     out=y[s][:],
                     lhsT=w2_words[:, g, cols].bitcast(FP8X4),
-                    lhsT_scale=w2_planes[row0:P, g % PER_PLANE, cols],
+                    lhsT_scale=w2_planes[plane // 2][4 * (plane % 2) : P, g % PER_PLANE, cols],
                     rhs=codes_of[g][:].bitcast(FP8X4),
                     rhs_scale=plane_of[g][:],
                     start=(g == 0),
@@ -267,38 +284,49 @@ def tile_waveletblock_k_kernel(
             if 1 <= i <= GROUPS:
                 quantise(i - 1, grouped)
 
+        halves = [slice(P * h, P * (h + 1)) for h in range(2)]
+        rows_half = IMAGES * HALF // 2
         z = keep.tile([P, SUBBANDS, TOKENS], F32)
-        for s in range(2):
-            nc.vector.tensor_scalar(
-                out=z[:, s, :],
-                in0=y[s][:],
-                scalar1=0.5,
-                scalar2=half_out_bias[:, s : s + 1],
-                op0=ALU.mult,
-                op1=ALU.add,
-            )
-            nc.scalar.activation(
-                out=z[:, 2 + s, :],
-                in_=y[2 + s][:],
-                func=ACT.Identity,
-                bias=half_out_bias[:, 2 + s : 3 + s],
-                scale=0.5,
-            )
+        for toks in halves:
+            for s in range(2):
+                nc.vector.tensor_scalar(
+                    out=z[:, s, toks],
+                    in0=y[s][:, toks],
+                    scalar1=0.5,
+                    scalar2=half_out_bias[:, s : s + 1],
+                    op0=ALU.mult,
+                    op1=ALU.add,
+                )
+                nc.scalar.activation(
+                    out=z[:, 2 + s, toks],
+                    in_=y[2 + s][:, toks],
+                    func=ACT.Identity,
+                    bias=half_out_bias[:, 2 + s : 3 + s],
+                    scale=0.5,
+                )
         first = keep.tile([P, 2, 2, TOKENS], F32)
-        nc.vector.tensor_tensor(out=first[:, 0], in0=z[:, 0:2, :], in1=z[:, 2:4, :], op=ALU.subtract)
-        nc.vector.tensor_tensor(out=first[:, 1], in0=z[:, 0:2, :], in1=z[:, 2:4, :], op=ALU.add)
+        for toks in halves:
+            for r, op in enumerate((ALU.subtract, ALU.add)):
+                nc.vector.tensor_tensor(out=first[:, r, :, toks], in0=z[:, 0:2, toks], in1=z[:, 2:4, toks], op=op)
         planar = keep.tile([P, IMAGES * HALF, 2, 2, HALF], F32)
-        left = first[:, :, 0, :].rearrange("p r (mi j) -> p r mi j", j=HALF)
-        right_half = first[:, :, 1, :].rearrange("p r (mi j) -> p r mi j", j=HALF)
         by_column = planar[:].rearrange("p mi r q j -> p q r mi j")
-        nc.vector.tensor_tensor(out=by_column[:, 0], in0=left, in1=right_half, op=ALU.subtract)
-        nc.vector.tensor_tensor(out=by_column[:, 1], in0=left, in1=right_half, op=ALU.add)
+        for h, toks in enumerate(halves):
+            rows = slice(rows_half * h, rows_half * (h + 1))
+            left = first[:, :, 0, toks].rearrange("p r (mi j) -> p r mi j", j=HALF)
+            right = first[:, :, 1, toks].rearrange("p r (mi j) -> p r mi j", j=HALF)
+            for q, op in enumerate((ALU.subtract, ALU.add)):
+                nc.vector.tensor_tensor(out=by_column[:, q, :, rows], in0=left, in1=right, op=op)
         rec = keep.tile([P, IMAGES * HALF * 2, HALF, 2], F32)
         woven = planar[:].rearrange("p mi r q j -> p (mi r) j q")
-        rows_half = IMAGES * HALF
-        nc.vector.tensor_copy(out=rec[:, 0:rows_half], in_=woven[:, 0:rows_half])
-        nc.scalar.copy(out=rec[:, rows_half : 2 * rows_half], in_=woven[:, rows_half : 2 * rows_half])
-        nc.sync.dma_start(
-            out=out.rearrange("b l c h w -> c (b l) (h w)"),
-            in_=rec[:].rearrange("p (m h) j q -> p m (h j q)", m=IMAGES),
-        )
+        to_store = out.rearrange("b l c h w -> c (b l) (h w)")
+        for h in range(2):
+            lo = 2 * rows_half * h
+            hi = 2 * rows_half * (h + 1)
+            split = lo if h == 0 else lo + (hi - lo) * 5 // 8
+            if split > lo:
+                nc.vector.tensor_copy(out=rec[:, lo:split], in_=woven[:, lo:split])
+            nc.scalar.copy(out=rec[:, split:hi], in_=woven[:, split:hi])
+            nc.sync.dma_start(
+                out=to_store[:, 2 * h : 2 * h + 2, :],
+                in_=rec[:, lo:hi].rearrange("p (m h) j q -> p m (h j q)", m=2),
+            )

@@ -30,6 +30,7 @@ PLANES = 4
 PER_PLANE = GROUPS // PLANES
 EARLY = 2
 LAG = 4
+WARM_UPS = 5
 AHEAD = 2
 
 FLOPS = 2 * 2 * TOKENS * K_PASS * HIDDEN
@@ -55,11 +56,10 @@ def tile_waveletblock_k_kernel(
         w2_planes = [
             keep.tile([P, PER_PLANE, K_PASS], U8, name="w2_planes%d" % j, align_bytes=64) for j in range(PLANES // 2)
         ]
-        nc.vector.memset(w1_raw_planes[:].bitcast(I32), 0)
-        nc.gpsimd.memset(bias_rows[:].bitcast(I32), 0)
-
         ident = keep.tile([P, P], BF16)
         make_identity(nc, ident[:])
+        nc.gpsimd.memset(w1_raw_planes[:].bitcast(I32), 0)
+        nc.gpsimd.memset(bias_rows[:].bitcast(I32), 0)
         for planes in w2_planes:
             nc.gpsimd.memset(planes[:].rearrange("p c n -> p (c n)").bitcast(I32), 0)
 
@@ -125,6 +125,8 @@ def tile_waveletblock_k_kernel(
 
         signs = keep.tile([P, 4, SUBBANDS, QUADS], BF16)
         haar = keep.tile([P, IMAGES, 4, P], BF16)
+        warm_src = keep.tile([P, P], BF16)
+        nc.vector.memset(warm_src[:], 0.5)
         nc.vector.memset(signs[:], 0.5)
         nc.vector.memset(signs[:, 0:2, 1, :], -0.5)
         nc.vector.memset(signs[:, 0:3:2, 2, :], -0.5)
@@ -137,7 +139,7 @@ def tile_waveletblock_k_kernel(
                 op=ALU.mult,
             )
         table_warm = keep.tile([P, 1], F32)
-        nc.scalar.activation(out=table_warm[:], in_=signs[:, 0, 0, 0:1], func=ACT.Silu)
+        nc.scalar.activation(out=table_warm[:], in_=warm_src[:, 0:1], func=ACT.Silu)
 
         w1_sorted = keep.tile([P, GROUPS, K_PASS], U32, align_bytes=64)
         w1_planes = keep.tile([P, PER_PLANE * K_PASS], U8, align_bytes=64)
@@ -159,35 +161,42 @@ def tile_waveletblock_k_kernel(
         sort_words(0)
         sort_planes(0)
 
+        warm = psum_first.tile([P, K_PASS], F32, name="warm", tag="first")
+        for step in range(WARM_UPS):
+            nc.tensor.matmul(
+                out=warm[:],
+                lhsT=warm_src[:],
+                rhs=warm_src[:].unsqueeze(1).to_broadcast([P, PACK, P]),
+                start=True,
+                stop=True,
+            )
         d_grouped = keep.tile([P, IMAGES, PIXELS, PACK], BF16, align_bytes=64)
         d_codes = keep.tile([P, TOKENS], U32, align_bytes=64)
         d_plane = keep.tile([P, TOKENS], U8, align_bytes=64)
         x_par = x_sb[:].rearrange("p (t i a j b) -> p a b t i j", t=PACK, i=HALF, a=2, j=HALF, b=2)
-        for pair in range(2):
-            d_acc = psum_second.tile([P, 2, PACK * PIXELS], F32, name="d_acc%d" % pair, tag="second")
-            for half in range(2):
-                for r in range(4):
-                    nc.tensor.matmul(
-                        out=d_acc[:, half, :],
-                        lhsT=haar[:, 2 * pair + half, r, :],
-                        rhs=x_par[:, r % 2, r // 2],
-                        start=(r == 0),
-                        stop=(r == 3),
-                    )
-            images = slice(2 * pair, 2 * pair + 2)
-            toks = slice(P * pair, P * (pair + 1))
-            by_token = d_acc[:].rearrange("p m (t k) -> p m k t", t=PACK)
-            if pair == 0:
-                nc.scalar.copy(out=d_grouped[:, images], in_=by_token)
+        for m in range(IMAGES):
+            d_acc = psum_second.tile([P, PACK * PIXELS], F32, name="d_acc%d" % m, tag="second")
+            for r in range(4):
+                nc.tensor.matmul(
+                    out=d_acc[:],
+                    lhsT=haar[:, m, r, :],
+                    rhs=x_par[:, r % 2, r // 2],
+                    start=(r == 0),
+                    stop=(r == 3),
+                )
+            by_token = d_acc[:].rearrange("p (t k) -> p k t", t=PACK)
+            if m % 2 == 0:
+                nc.scalar.copy(out=d_grouped[:, m], in_=by_token)
             else:
-                nc.vector.tensor_copy(out=d_grouped[:, images], in_=by_token)
-            nc.vector.quantize_mx(
-                out=d_codes[:, toks].bitcast(FP8X4),
-                scales=d_plane[:, toks],
-                in_=d_grouped[:, images].rearrange("p m k t -> p (m k t)"),
-            )
+                nc.vector.tensor_copy(out=d_grouped[:, m], in_=by_token)
+                toks = slice(PIXELS * (m - 1), PIXELS * (m + 1))
+                nc.vector.quantize_mx(
+                    out=d_codes[:, toks].bitcast(FP8X4),
+                    scales=d_plane[:, toks],
+                    in_=d_grouped[:, m - 1 : m + 1].rearrange("p m k t -> p (m k t)"),
+                )
 
-        bias_flip = psum_second.tile([P, PACK + 1, P], BF16, name="bias_flip", tag="second")
+        bias_flip = psum_first.tile([P, PACK + 1, P], BF16, name="bias_flip", tag="first")
         for t in range(PACK):
             nc.tensor.transpose(
                 out=bias_flip[:, t, :],
@@ -199,6 +208,11 @@ def tile_waveletblock_k_kernel(
         half_out_bias = keep.tile([P, SUBBANDS], F32)
         nc.scalar.copy(out=bias[:], in_=bias_flip[:, 0:PACK, 0:GROUPS])
         nc.scalar.mul(half_out_bias[:], bias_flip[:, PACK, 0:SUBBANDS], 0.5)
+        z_bias = keep.tile([P, 2, 2], F32)
+        for r, op in enumerate((ALU.subtract, ALU.add)):
+            nc.vector.tensor_tensor(
+                out=z_bias[:, r, :], in0=half_out_bias[:, 0:2], in1=half_out_bias[:, 2:4], op=op
+            )
 
         planar_of = {}
         codes_of = {}
@@ -286,28 +300,29 @@ def tile_waveletblock_k_kernel(
 
         halves = [slice(P * h, P * (h + 1)) for h in range(2)]
         rows_half = IMAGES * HALF // 2
-        z = keep.tile([P, SUBBANDS, TOKENS], F32)
-        for toks in halves:
-            for s in range(2):
-                nc.vector.tensor_scalar(
-                    out=z[:, s, toks],
-                    in0=y[s][:, toks],
-                    scalar1=0.5,
-                    scalar2=half_out_bias[:, s : s + 1],
-                    op0=ALU.mult,
-                    op1=ALU.add,
-                )
-                nc.scalar.activation(
-                    out=z[:, 2 + s, toks],
-                    in_=y[2 + s][:, toks],
-                    func=ACT.Identity,
-                    bias=half_out_bias[:, 2 + s : 3 + s],
-                    scale=0.5,
-                )
+        z = keep.tile([P, 2, 2, TOKENS], F32)
         first = keep.tile([P, 2, 2, TOKENS], F32)
         for toks in halves:
-            for r, op in enumerate((ALU.subtract, ALU.add)):
-                nc.vector.tensor_tensor(out=first[:, r, :, toks], in0=z[:, 0:2, toks], in1=z[:, 2:4, toks], op=op)
+            for s in range(2):
+                for r in range(2):
+                    nc.scalar.activation(
+                        out=z[:, r, s, toks],
+                        in_=y[s][:, toks],
+                        func=ACT.Identity,
+                        bias=z_bias[:, r, s : s + 1],
+                        scale=0.5,
+                    )
+        for toks in halves:
+            for s in range(2):
+                for r in range(2):
+                    nc.vector.scalar_tensor_tensor(
+                        out=first[:, r, s, toks],
+                        in0=y[2 + s][:, toks],
+                        scalar=-0.5 if r == 0 else 0.5,
+                        in1=z[:, r, s, toks],
+                        op0=ALU.mult,
+                        op1=ALU.add,
+                    )
         planar = keep.tile([P, IMAGES * HALF, 2, 2, HALF], F32)
         by_column = planar[:].rearrange("p mi r q j -> p q r mi j")
         for h, toks in enumerate(halves):

@@ -147,8 +147,8 @@ def tile_waveletblock_k_kernel(
         def sort_words(g):
             lo = K_PASS * (g % CHUNK)
             nc.vector.tensor_copy(
-                out=w1_sorted[:, g, :].bitcast(I32).rearrange("p (t m) -> p m t", t=PACK),
-                in_=w1_raw[g // CHUNK][:, lo : lo + K_PASS].bitcast(I32).rearrange("p (m t) -> p m t", t=PACK),
+                out=w1_sorted[:, g, :].bitcast(I32).rearrange("p (t m i) -> p m t i", t=PACK, i=2),
+                in_=w1_raw[g // CHUNK][:, lo : lo + K_PASS].bitcast(I32).rearrange("p (m i t) -> p m t i", t=PACK, i=2),
             )
 
         def sort_planes(piece):

@@ -29,7 +29,8 @@ LOAD = 2
 PLANES = 4
 PER_PLANE = GROUPS // PLANES
 EARLY = 2
-LAG = 4
+LEAD = 8
+LAG = 6
 WARM_UPS = 5
 AHEAD = 2
 
@@ -113,6 +114,7 @@ def tile_waveletblock_k_kernel(
         load_w1(2, 2)
         load_w1_planes(EARLY, PER_PLANE - EARLY)
         load_w1(4, 2)
+        load_w1(6, 2)
         load_w2_planes(0)
         load_w2_planes(1)
         for g in range(0, GROUPS, LOAD):
@@ -120,8 +122,8 @@ def tile_waveletblock_k_kernel(
                 load_w2_planes(2)
                 load_w2_planes(3)
             load_w2(g, LOAD)
-            if g + 6 < GROUPS:
-                load_w1(g + 6, LOAD)
+            if g + LEAD < GROUPS:
+                load_w1(g + LEAD, LOAD)
 
         signs = keep.tile([P, 4, SUBBANDS, QUADS], BF16)
         haar = keep.tile([P, IMAGES, 4, P], BF16)

from contextlib import ExitStack

import concourse.mybir as mybir
from concourse.masks import make_identity

F32 = mybir.dt.float32
BF16 = mybir.dt.bfloat16
I32 = mybir.dt.int32
U32 = mybir.dt.uint32
U8 = mybir.dt.uint8
FP8X4 = mybir.dt.float8_e4m3fn_x4
ALU = mybir.AluOpType
ACT = mybir.ActivationFunctionType

P = 128
PACK = 4
K_PASS = P * PACK
IMAGES = 4
CHANNELS = 128
QUADS = CHANNELS // PACK
HALF = 8
PIXELS = HALF * HALF
TOKENS = IMAGES * PIXELS
HIDDEN = 16384
GROUPS = HIDDEN // K_PASS
SUBBANDS = 4
CHUNK = 4
LOAD = 2
PLANES = 4
PER_PLANE = GROUPS // PLANES
EARLY = 2
LEAD = 8
LAG = 6
WARM_UPS = 5
AHEAD = 2

FLOPS = 2 * 2 * TOKENS * K_PASS * HIDDEN


def tile_waveletblock_k_kernel(
    tc, x, conv_w_words, conv_w_scales, conv_b, conv_out_w_words, conv_out_w_scales, conv_out_b, out
):
    nc = tc.nc
    with ExitStack() as ctx:
        keep = ctx.enter_context(tc.tile_pool(name="keep", bufs=1))
        raws = ctx.enter_context(tc.tile_pool(name="raws", bufs=4))
        planars = ctx.enter_context(tc.tile_pool(name="planars", bufs=3))
        groupeds = ctx.enter_context(tc.tile_pool(name="groupeds", bufs=3))
        quantised = ctx.enter_context(tc.tile_pool(name="quantised", bufs=LAG + 1))
        psum_first = ctx.enter_context(tc.psum_pool(name="psum_first", bufs=4))
        psum_second = ctx.enter_context(tc.psum_pool(name="psum_second", bufs=SUBBANDS))
        ctx.enter_context(tc.manual_schedule())

        x_sb = keep.tile([P, PACK * 4 * PIXELS], BF16)
        bias_rows = keep.tile([P, K_PASS + P], BF16)
        w1_raw_planes = keep.tile([P, PER_PLANE * K_PASS], U8, align_bytes=64)
        w2_planes = [
            keep.tile([P, PER_PLANE, K_PASS], U8, name="w2_planes%d" % j, align_bytes=64) for j in range(PLANES // 2)
        ]
        ident = keep.tile([P, P], BF16)
        make_identity(nc, ident[:])
        nc.gpsimd.memset(w1_raw_planes[:].bitcast(I32), 0)
        nc.gpsimd.memset(bias_rows[:].bitcast(I32), 0)
        for planes in w2_planes:
            nc.gpsimd.memset(planes[:].rearrange("p c n -> p (c n)").bitcast(I32), 0)

        nc.sync.dma_start(out=x_sb[:], in_=x.rearrange("b l (q t) h w -> (b l q) (t h w)", t=PACK))
        w1_flat = conv_w_words[0].rearrange("p n t -> p (n t)")
        w1_raw = []
        w2_words = keep.tile([P, GROUPS, K_PASS], U32, align_bytes=64)

        def load_w1(g, count):
            if g % CHUNK == 0:
                w1_raw.append(raws.tile([P, CHUNK * K_PASS], U32, name="w1_raw%d" % g, tag="w1_raw", align_bytes=64))
            first = K_PASS * (g % CHUNK)
            nc.sync.dma_start(
                out=w1_raw[g // CHUNK][:, first : first + K_PASS * count].bitcast(I32),
                in_=w1_flat[:, 4 * K_PASS * g : 4 * K_PASS * (g + count)].bitcast(I32),
            )

        def load_w2(g, count):
            nc.sync.dma_start(
                out=w2_words[:, g : g + count, :].bitcast(I32),
                in_=conv_out_w_words[g : g + count].rearrange("g p n t -> p g (n t)").bitcast(I32),
            )

        def load_w1_planes(first, count):
            cols = slice(K_PASS * first, K_PASS * (first + count))
            for quad in range(4):
                nc.sync.dma_start(
                    out=w1_raw_planes[32 * quad : 32 * quad + 16, cols].bitcast(I32),
                    in_=conv_w_scales[0, 4 * quad : 4 * quad + 4, :]
                    .rearrange("r (k c) -> k r c", k=PLANES)[:, :, cols]
                    .bitcast(I32),
                )

        def load_w2_planes(k):
            row0 = 4 * (k % 2)
            for quad in range(4):
                nc.sync.dma_start(
                    out=w2_planes[k // 2][32 * quad + row0 : 32 * quad + row0 + 4, :, :].bitcast(I32),
                    in_=conv_out_w_scales[PER_PLANE * k : PER_PLANE * (k + 1), 4 * quad : 4 * quad + 4, :]
                    .rearrange("g r n -> r g n")
                    .bitcast(I32),
                )

        load_w1(0, 1)
        load_w1_planes(0, EARLY)
        nc.sync.dma_start(out=bias_rows[0:GROUPS, 0:K_PASS], in_=conv_b.rearrange("(g c) -> g c", c=K_PASS))
        nc.sync.dma_start(
            out=bias_rows[0:SUBBANDS, K_PASS : K_PASS + P], in_=conv_out_b.rearrange("(s c) -> s c", c=CHANNELS)
        )
        load_w1(1, 1)
        load_w1(2, 2)
        load_w1_planes(EARLY, PER_PLANE - EARLY)
        load_w1(4, 2)
        load_w1(6, 2)
        load_w2_planes(0)
        load_w2_planes(1)
        for g in range(0, GROUPS, LOAD):
            if g == PER_PLANE:
                load_w2_planes(2)
                load_w2_planes(3)
            load_w2(g, LOAD)
            if g + LEAD < GROUPS:
                load_w1(g + LEAD, LOAD)

        signs = keep.tile([P, 4, SUBBANDS, QUADS], BF16)
        haar = keep.tile([P, IMAGES, 4, P], BF16)
        warm_src = keep.tile([P, P], BF16)
        nc.vector.memset(warm_src[:], 0.5)
        nc.vector.memset(signs[:], 0.5)
        nc.vector.memset(signs[:, 0:2, 1, :], -0.5)
        nc.vector.memset(signs[:, 0:3:2, 2, :], -0.5)
        nc.vector.memset(signs[:, 1:3, 3, :], -0.5)
        for m in range(IMAGES):
            nc.vector.tensor_tensor(
                out=haar[:, m].rearrange("p r (s q) -> p (r s) q", q=QUADS),
                in0=signs[:].rearrange("p r s q -> p (r s) q"),
                in1=ident[:, QUADS * m : QUADS * (m + 1)].unsqueeze(1).to_broadcast([P, 4 * SUBBANDS, QUADS]),
                op=ALU.mult,
            )
        table_warm = keep.tile([P, 1], F32)
        nc.scalar.activation(out=table_warm[:], in_=warm_src[:, 0:1], func=ACT.Silu)

        w1_sorted = keep.tile([P, GROUPS, K_PASS], U32, align_bytes=64)
        w1_planes = keep.tile([P, PER_PLANE * K_PASS], U8, align_bytes=64)

        def sort_words(g):
            lo = K_PASS * (g % CHUNK)
            nc.vector.tensor_copy(
                out=w1_sorted[:, g, :].bitcast(I32).rearrange("p (t m i) -> p m t i", t=PACK, i=2),
                in_=w1_raw[g // CHUNK][:, lo : lo + K_PASS].bitcast(I32).rearrange("p (m i t) -> p m t i", t=PACK, i=2),
            )

        def sort_planes(piece):
            cols = slice(K_PASS * piece, K_PASS * (piece + 1))
            nc.vector.tensor_copy(
                out=w1_planes[:, cols].rearrange("p (t m) -> p t m", t=PACK),
                in_=w1_raw_planes[:, cols].rearrange("p (m t) -> p t m", t=PACK),
            )

        sort_words(0)
        sort_planes(0)

        warm = psum_first.tile([P, K_PASS], F32, name="warm", tag="first")
        for step in range(WARM_UPS):
            nc.tensor.matmul(
                out=warm[:],
                lhsT=warm_src[:],
                rhs=warm_src[:].unsqueeze(1).to_broadcast([P, PACK, P]),
                start=True,
                stop=True,
            )
        d_grouped = keep.tile([P, IMAGES, PIXELS, PACK], BF16, align_bytes=64)
        d_codes = keep.tile([P, TOKENS], U32, align_bytes=64)
        d_plane = keep.tile([P, TOKENS], U8, align_bytes=64)
        x_par = x_sb[:].rearrange("p (t i a j b) -> p a b t i j", t=PACK, i=HALF, a=2, j=HALF, b=2)
        for m in range(IMAGES):
            d_acc = psum_second.tile([P, PACK * PIXELS], F32, name="d_acc%d" % m, tag="second")
            for r in range(4):
                nc.tensor.matmul(
                    out=d_acc[:],
                    lhsT=haar[:, m, r, :],
                    rhs=x_par[:, r % 2, r // 2],
                    start=(r == 0),
                    stop=(r == 3),
                )
            by_token = d_acc[:].rearrange("p (t k) -> p k t", t=PACK)
            if m % 2 == 0:
                nc.scalar.copy(out=d_grouped[:, m], in_=by_token)
            else:
                nc.vector.tensor_copy(out=d_grouped[:, m], in_=by_token)
                toks = slice(PIXELS * (m - 1), PIXELS * (m + 1))
                nc.vector.quantize_mx(
                    out=d_codes[:, toks].bitcast(FP8X4),
                    scales=d_plane[:, toks],
                    in_=d_grouped[:, m - 1 : m + 1].rearrange("p m k t -> p (m k t)"),
                )

        bias_flip = psum_first.tile([P, PACK + 1, P], BF16, name="bias_flip", tag="first")
        for t in range(PACK):
            nc.tensor.transpose(
                out=bias_flip[:, t, :],
                in_=bias_rows[:, 0:K_PASS].rearrange("g (p t) -> g t p", t=PACK)[:, t],
                identity=ident[:],
            )
        nc.tensor.transpose(out=bias_flip[:, PACK, :], in_=bias_rows[:, K_PASS : K_PASS + P], identity=ident[:])
        bias = keep.tile([P, PACK, GROUPS], F32)
        half_out_bias = keep.tile([P, SUBBANDS], F32)
        nc.scalar.copy(out=bias[:], in_=bias_flip[:, 0:PACK, 0:GROUPS])
        nc.scalar.mul(half_out_bias[:], bias_flip[:, PACK, 0:SUBBANDS], 0.5)
        z_bias = keep.tile([P, 2, 2], F32)
        for r, op in enumerate((ALU.subtract, ALU.add)):
            nc.vector.tensor_tensor(
                out=z_bias[:, r, :], in0=half_out_bias[:, 0:2], in1=half_out_bias[:, 2:4], op=op
            )

        planar_of = {}
        codes_of = {}
        plane_of = {}
        y = []

        def first_matmul(g, pair):
            row0 = 4 * (g // PER_PLANE)
            acc = psum_first.tile([P, 2, TOKENS], F32, tag="first")
            for half in range(2):
                t = 2 * pair + half
                cols = slice(P * t, P * (t + 1))
                plane_cols = slice(K_PASS * (g % PER_PLANE) + P * t, K_PASS * (g % PER_PLANE) + P * (t + 1))
                nc.tensor.matmul_mx(
                    out=acc[:, half, :],
                    lhsT=w1_sorted[:, g, cols].bitcast(FP8X4),
                    lhsT_scale=w1_planes[row0:P, plane_cols],
                    rhs=d_codes[:].bitcast(FP8X4),
                    rhs_scale=d_plane[:],
                    start=True,
                    stop=True,
                )
            if pair == 0:
                planar_of[g] = planars.tile([P, PACK, TOKENS], BF16, name="planar", tag="planar")
            for half in range(2):
                t = 2 * pair + half
                nc.scalar.activation(
                    out=planar_of[g][:, t, :], in_=acc[:, half, :], func=ACT.Silu, bias=bias[:, t, g : g + 1]
                )

        def interleave(g):
            grouped = groupeds.tile([P, TOKENS, PACK], BF16, name="grouped", tag="grouped", align_bytes=64)
            nc.vector.tensor_copy(
                out=grouped[:].rearrange("p (c i) t -> p c t i", i=4),
                in_=planar_of[g][:].rearrange("p t (c i) -> p c t i", i=4),
            )
            return grouped

        def quantise(g, grouped):
            codes = quantised.tile([P, TOKENS], U32, name="codes", tag="codes", align_bytes=64)
            plane = quantised.tile([P, TOKENS], U8, name="plane", tag="plane", align_bytes=64)
            nc.vector.quantize_mx(
                out=codes[:].bitcast(FP8X4), scales=plane[:], in_=grouped[:].rearrange("p k t -> p (k t)")
            )
            codes_of[g] = codes
            plane_of[g] = plane

        def second_matmul(g, tiles):
            plane = g // PER_PLANE
            for s in tiles:
                cols = slice(P * s, P * (s + 1))
                nc.tensor.matmul_mx(
                    out=y[s][:],
                    lhsT=w2_words[:, g, cols].bitcast(FP8X4),
                    lhsT_scale=w2_planes[plane // 2][4 * (plane % 2) : P, g % PER_PLANE, cols],
                    rhs=codes_of[g][:].bitcast(FP8X4),
                    rhs_scale=plane_of[g][:],
                    start=(g == 0),
                    stop=(g == GROUPS - 1),
                )

        for g in range(1, AHEAD):
            sort_words(g)
            sort_planes(g)
        for i in range(GROUPS + LAG):
            if i == LAG:
                for s in range(SUBBANDS):
                    y.append(psum_second.tile([P, TOKENS], F32, name="y%d" % s, tag="second"))
            if i < GROUPS:
                first_matmul(i, 0)
            if i >= LAG:
                second_matmul(i - LAG, (0, 1))
            if i < GROUPS:
                first_matmul(i, 1)
            if i >= LAG:
                second_matmul(i - LAG, (2, 3))
            if 1 <= i <= GROUPS:
                grouped = interleave(i - 1)
            if i + AHEAD < PER_PLANE:
                sort_planes(i + AHEAD)
            if i + AHEAD < GROUPS:
                sort_words(i + AHEAD)
            if 1 <= i <= GROUPS:
                quantise(i - 1, grouped)

        halves = [slice(P * h, P * (h + 1)) for h in range(2)]
        rows_half = IMAGES * HALF // 2
        z = keep.tile([P, 2, 2, TOKENS], F32)
        first = keep.tile([P, 2, 2, TOKENS], F32)
        for toks in halves:
            for s in range(2):
                for r in range(2):
                    nc.scalar.activation(
                        out=z[:, r, s, toks],
                        in_=y[s][:, toks],
                        func=ACT.Identity,
                        bias=z_bias[:, r, s : s + 1],
                        scale=0.5,
                    )
        for toks in halves:
            for s in range(2):
                for r in range(2):
                    nc.vector.scalar_tensor_tensor(
                        out=first[:, r, s, toks],
                        in0=y[2 + s][:, toks],
                        scalar=-0.5 if r == 0 else 0.5,
                        in1=z[:, r, s, toks],
                        op0=ALU.mult,
                        op1=ALU.add,
                    )
        planar = keep.tile([P, IMAGES * HALF, 2, 2, HALF], F32)
        by_column = planar[:].rearrange("p mi r q j -> p q r mi j")
        for h, toks in enumerate(halves):
            rows = slice(rows_half * h, rows_half * (h + 1))
            left = first[:, :, 0, toks].rearrange("p r (mi j) -> p r mi j", j=HALF)
            right = first[:, :, 1, toks].rearrange("p r (mi j) -> p r mi j", j=HALF)
            for q, op in enumerate((ALU.subtract, ALU.add)):
                nc.vector.tensor_tensor(out=by_column[:, q, :, rows], in0=left, in1=right, op=op)
        rec = keep.tile([P, IMAGES * HALF * 2, HALF, 2], F32)
        woven = planar[:].rearrange("p mi r q j -> p (mi r) j q")
        to_store = out.rearrange("b l c h w -> c (b l) (h w)")
        for h in range(2):
            lo = 2 * rows_half * h
            hi = 2 * rows_half * (h + 1)
            split = lo if h == 0 else lo + (hi - lo) * 5 // 8
            if split > lo:
                nc.vector.tensor_copy(out=rec[:, lo:split], in_=woven[:, lo:split])
            nc.scalar.copy(out=rec[:, split:hi], in_=woven[:, split:hi])
            nc.sync.dma_start(
                out=to_store[:, 2 * h : 2 * h + 2, :],
                in_=rec[:, lo:hi].rearrange("p (m h) j q -> p m (h j q)", m=2),
            )
